import numpy as np
import ml_dtypes


def mxq(x, axis, fmt="e4m3"):
    dtype, down = {"e4m3": (ml_dtypes.float8_e4m3fn, 7), "e5m2": (ml_dtypes.float8_e5m2, 14)}[fmt]
    v = np.moveaxis(np.asarray(x, np.float32).astype(ml_dtypes.bfloat16).astype(np.float64), axis, -1)
    blocks = v.reshape(v.shape[:-1] + (-1, 32))
    amax = np.abs(blocks).max(-1, keepdims=True)
    byte = np.maximum(np.where(amax > 0, np.frexp(amax)[1] - 1 + 127, 0) - down, 1)
    scale = np.exp2(byte - 127.0)
    codes = (blocks / scale).astype(np.float32).astype(dtype).astype(np.float64)
    return np.moveaxis((codes * scale).reshape(v.shape), -1, axis)


WIDE = False


def mx_kscale(k):
    if not WIDE:
        return np.ones(k)
    levels = np.array([10, -10, 5, -5, 0])
    a = np.random.permutation(np.resize(levels, k // 512 * 4)).reshape(k // 512, 4)
    idx = np.arange(k)
    return np.exp2(a[idx // 512, idx % 128 // 32])


BF16 = ml_dtypes.bfloat16


def bf(x):
    return np.asarray(x, np.float32).astype(BF16)


def f64(x):
    return np.asarray(x).astype(np.float64)


B, N, D, O, M = 16, 512, 128, 512, 4
KW = D * M


def draw_support():
    m = np.exp(2.0 * np.random.standard_normal((N, N)) - 2.0) * (3.0 / N) + np.eye(N)
    d = m.sum(axis=1) ** -0.5
    return (m * d[None, :]).T * d[None, :]


def setup_inputs():
    u = mx_kscale(KW)[::M]
    return {"x0": bf(np.random.standard_normal((B, N, D)) * u),
            "x1": bf(np.random.standard_normal((B, N, D)) * 0.4 * u),
            "x2": bf(np.random.standard_normal((B, N, D)) * 0.9 * u),
            "support": bf(draw_support()),
            "weights": bf(np.random.standard_normal((KW, O)) / np.sqrt(KW) / np.repeat(u, M)[:, None]),
            "biases": bf(np.random.standard_normal(O) * 0.3)}


def reference(x0, x1, x2, support, weights, biases):
    x0, x1, x2 = f64(x0), f64(x1), f64(x2)
    x3 = 2.0 * (mxq(f64(support), 1, "e4m3") @ mxq(x2, 1, "e4m3")) - x1
    x = np.stack([x0, x1, x2, x3], axis=-1).reshape(B * N, KW)
    out = (mxq(x, 1, "e4m3") @ mxq(f64(weights), 0, "e4m3")) + f64(biases)
    return out.reshape(B, N, O)

@@ -1,0 +1,227 @@
+from contextlib import ExitStack
+
+import concourse.mybir as mybir
+from concourse.masks import make_identity
+
+F32 = mybir.dt.float32
+BF16 = mybir.dt.bfloat16
+U32 = mybir.dt.uint32
+U8 = mybir.dt.uint8
+FP8X4 = mybir.dt.float8_e4m3fn_x4
+ALU = mybir.AluOpType
+
+P = 128
+B, N, D, O, M = 16, 512, 128, 512, 4
+T = N // P
+FLOPS = 2 * B * N * N * D + 2 * B * N * (D * M) * O
+
+CHUNKS = [(0, 1), (1, 1), (2, 2), (4, 4), (8, 4), (12, 4)]
+PIN = False
+GP_EVEN = (3,)
+GP_ODD = (3,)
+
+
+def tile_dgcn_pb_t_kernel(tc, x0, x1, x2, support, weights, biases, out):
+    nc = tc.nc
+    xs_dram = [x0, x1, x2]
+    chunk_of = {}
+    for c, (b0, nb) in enumerate(CHUNKS):
+        for bi in range(nb):
+            chunk_of[b0 + bi] = (c, bi)
+
+    with ExitStack() as ctx:
+        const = ctx.enter_context(tc.tile_pool(name="const", bufs=1))
+        work = ctx.enter_context(tc.tile_pool(name="work", bufs=3))
+        outp = ctx.enter_context(tc.tile_pool(name="outp", bufs=4))
+        ps1 = ctx.enter_context(tc.psum_pool(name="ps1", bufs=2))
+        pst = ctx.enter_context(tc.psum_pool(name="pst", bufs=2))
+        ps2 = ctx.enter_context(tc.psum_pool(name="ps2", bufs=4))
+        if PIN:
+            ctx.enter_context(tc.manual_schedule())
+
+        sup_sb = const.tile([P, T * N], BF16)
+        nc.sync.dma_start(out=sup_sb[:], in_=support.rearrange("(p t) j -> p (t j)", t=T))
+        x_sb = {}
+
+        def load_x(m, c):
+            b0, nb = CHUNKS[c]
+            xt = const.tile([P, nb, T * D], BF16, name="x%d_c%d" % (m, c))
+            nc.sync.dma_start(
+                out=xt[:], in_=xs_dram[m][b0 : b0 + nb].rearrange("b (p t) d -> p b (t d)", t=T)
+            )
+            x_sb[(m, c)] = xt
+
+        w_sb = const.tile([P, M * O], BF16)
+        bias_rows = const.tile([P, O], BF16)
+        nc.vector.memset(bias_rows[:], 0.0)
+        for c in range(len(CHUNKS)):
+            load_x(2, c)
+            load_x(1, c)
+            load_x(0, c)
+            if c == 1:
+                nc.sync.dma_start(out=w_sb[:], in_=weights.rearrange("(p j) o -> p (j o)", j=M))
+                nc.sync.dma_start(out=bias_rows[0:1, :], in_=biases.rearrange("(a o) -> a o", a=1))
+
+        ident_f = const.tile([P, P], F32)
+        make_identity(nc, ident_f[:])
+        ident_b = const.tile([P, P], BF16)
+        make_identity(nc, ident_b[:])
+        ones_b = const.tile([P, P], BF16)
+        nc.vector.memset(ones_b[:], 1.0)
+
+        sg = const.tile([P, N * 4], BF16, align_bytes=64)
+        s_codes = const.tile([P, N], U32, align_bytes=64)
+        s_scales = const.tile([P, N], U8, align_bytes=64)
+        sup_w = sup_sb[:].bitcast(F32).rearrange("p (t i u) -> p t u i", t=T, u=2)
+        sg_w = sg[:].bitcast(F32).rearrange("p (c u) -> p c u", u=2)
+        for h in range(2):
+            sps = ps2.tile([P, 2, 2 * P], F32, name="sps", tag="acc2")
+            for tt in range(2):
+                for u in range(2):
+                    nc.tensor.transpose(
+                        sps[:, u, tt * P : (tt + 1) * P], sup_w[:, 2 * h + tt, u, :], ident_f[:]
+                    )
+            src = sps[:].rearrange("p u c -> p c u")
+            dst = sg_w[:, h * 2 * P : (h + 1) * 2 * P, :]
+            if h == 0:
+                nc.vector.tensor_copy(out=dst, in_=src)
+            else:
+                nc.scalar.copy(out=dst, in_=src)
+        nc.vector.quantize_mx(out=s_codes[:].bitcast(FP8X4), scales=s_scales[:], in_=sg[:])
+
+        x2c = {}
+        x2s = {}
+
+        def prepare_x2(c):
+            b0, nb = CHUNKS[c]
+            x2g = const.tile([P, nb, D, T], BF16, name="x2g_c%d" % c, align_bytes=64)
+            nc.gpsimd.tensor_scalar(
+                out=x2g[:],
+                in0=x_sb[(2, c)][:].rearrange("p b (t d) -> p b d t", t=T),
+                scalar1=1.0,
+                scalar2=0.0,
+                op0=ALU.mult,
+                op1=ALU.add,
+            )
+            codes = const.tile([P, nb * D], U32, name="x2c_c%d" % c, align_bytes=64)
+            scales = const.tile([P, nb * D], U8, name="x2s_c%d" % c, align_bytes=64)
+            nc.vector.quantize_mx(
+                out=codes[:].bitcast(FP8X4),
+                scales=scales[:],
+                in_=x2g[:].rearrange("p b d t -> p (b d t)"),
+            )
+            x2c[c] = codes
+            x2s[c] = scales
+
+        wg = const.tile([P, O * M], BF16, align_bytes=64)
+        w_codes = const.tile([P, O], U32, align_bytes=64)
+        w_scales = const.tile([P, O], U8, align_bytes=64)
+        bias_sb = const.tile([P, O], F32)
+
+        def prepare_weights():
+            nc.vector.tensor_copy(
+                out=wg[:].rearrange("p (o j) -> p o j", j=M),
+                in_=w_sb[:].rearrange("p (j o) -> p o j", j=M),
+            )
+            nc.vector.quantize_mx(out=w_codes[:].bitcast(FP8X4), scales=w_scales[:], in_=wg[:])
+            bps = ps2.tile([P, O], F32, name="bps", tag="acc2")
+            nc.tensor.matmul(bps[:], lhsT=ones_b[:], rhs=bias_rows[:], start=True, stop=True)
+            nc.scalar.copy(out=bias_sb[:], in_=bps[:])
+
+        x3_t = {}
+        xg_t = {}
+        xq_t = {}
+
+        def stage1(b):
+            c, bi = chunk_of[b]
+            acc1 = ps1.tile([P, T * D], F32, name="acc1", tag="acc1")
+            for t in range(T):
+                nc.tensor.matmul_mx(
+                    out=acc1[:, t * D : (t + 1) * D],
+                    lhsT=s_codes[:, t * P : (t + 1) * P].bitcast(FP8X4),
+                    lhsT_scale=s_scales[:, t * P : (t + 1) * P],
+                    rhs=x2c[c][:, bi * D : (bi + 1) * D].bitcast(FP8X4),
+                    rhs_scale=x2s[c][:, bi * D : (bi + 1) * D],
+                    start=True,
+                    stop=True,
+                )
+            x3 = work.tile([P, T * D], BF16, name="x3", tag="x3")
+            nc.vector.scalar_tensor_tensor(
+                out=x3[:],
+                in0=acc1[:],
+                scalar=2.0,
+                in1=x_sb[(1, c)][:, bi, :],
+                op0=ALU.mult,
+                op1=ALU.subtract,
+            )
+            x3_t[b] = x3
+
+        def transposes(b):
+            c, bi = chunk_of[b]
+            xg = work.tile([P, N, M], BF16, name="xg", tag="xg", align_bytes=64)
+            for h in range(2):
+                tp = pst.tile([P, M, 2 * P], BF16, name="tp", tag="tp")
+                for m in range(M):
+                    for tt in range(2):
+                        t = 2 * h + tt
+                        if m < 3:
+                            src = x_sb[(m, c)][:, bi, t * D : (t + 1) * D]
+                        else:
+                            src = x3_t[b][:, t * D : (t + 1) * D]
+                        nc.tensor.transpose(tp[:, m, tt * P : (tt + 1) * P], src, ident_b[:])
+                nc.scalar.copy(
+                    out=xg[:, h * 2 * P : (h + 1) * 2 * P, :], in_=tp[:].rearrange("p m c -> p c m")
+                )
+            xg_t[b] = xg
+
+        def quantise_x(b):
+            xc = work.tile([P, N], U32, name="xc", tag="xc", align_bytes=64)
+            xsc = work.tile([P, N], U8, name="xsc", tag="xsc", align_bytes=64)
+            nc.vector.quantize_mx(
+                out=xc[:].bitcast(FP8X4), scales=xsc[:], in_=xg_t[b][:].rearrange("p c m -> p (c m)")
+            )
+            xq_t[b] = (xc, xsc)
+
+        def stage2(b):
+            xc, xsc = xq_t[b]
+            gp_banks = GP_ODD if b % 2 else GP_EVEN
+            accs = []
+            for t in range(T):
+                acc2 = ps2.tile([P, O], F32, name="acc2", tag="acc2")
+                nc.tensor.matmul_mx(
+                    out=acc2[:],
+                    lhsT=xc[:, t * P : (t + 1) * P].bitcast(FP8X4),
+                    lhsT_scale=xsc[:, t * P : (t + 1) * P],
+                    rhs=w_codes[:].bitcast(FP8X4),
+                    rhs_scale=w_scales[:],
+                    start=True,
+                    stop=True,
+                )
+                accs.append(acc2)
+            res = outp.tile([P, T, O], F32, name="res", tag="res")
+            for t in range(T):
+                if t in gp_banks:
+                    tmp = work.tile([P, O], F32, name="tmp", tag="tmp")
+                    nc.scalar.copy(out=tmp[:], in_=accs[t][:])
+                    nc.gpsimd.tensor_tensor(out=res[:, t, :], in0=tmp[:], in1=bias_sb[:], op=ALU.add)
+                else:
+                    nc.vector.tensor_tensor(out=res[:, t, :], in0=accs[t][:], in1=bias_sb[:], op=ALU.add)
+            nc.sync.dma_start(out=out[b].rearrange("(p t) o -> p t o", t=T), in_=res[:])
+
+        prepare_x2(0)
+        prepare_x2(1)
+        next_chunk = 2
+        for i in range(B + 3):
+            if next_chunk < len(CHUNKS) and CHUNKS[next_chunk][0] <= i + 3:
+                prepare_x2(next_chunk)
+                next_chunk += 1
+            if i == 1:
+                prepare_weights()
+            if i < B:
+                stage1(i)
+            if 0 <= i - 1 < B:
+                transposes(i - 1)
+            if 0 <= i - 2 < B:
+                quantise_x(i - 2)
+            if 0 <= i - 3 < B:
+                stage2(i - 3)

@@ -16,9 +16,15 @@ T = N // P
 FLOPS = 2 * B * N * N * D + 2 * B * N * (D * M) * O
 
 CHUNKS = [(0, 1), (1, 1), (2, 2), (4, 4), (8, 4), (12, 4)]
-PIN = False
-GP_EVEN = (3,)
-GP_ODD = (3,)
+HEAD_B = 4
+
+
+def gp_banks(b):
+    return (0,)
+
+
+def f_on_vector(b, h):
+    return b < 2 and h == 0
 
 
 def tile_dgcn_pb_t_kernel(tc, x0, x1, x2, support, weights, biases, out):
@@ -33,14 +39,11 @@ def tile_dgcn_pb_t_kernel(tc, x0, x1, x2, support, weights, biases, out):
         const = ctx.enter_context(tc.tile_pool(name="const", bufs=1))
         work = ctx.enter_context(tc.tile_pool(name="work", bufs=3))
         outp = ctx.enter_context(tc.tile_pool(name="outp", bufs=4))
-        ps1 = ctx.enter_context(tc.psum_pool(name="ps1", bufs=2))
-        pst = ctx.enter_context(tc.psum_pool(name="pst", bufs=2))
+        ps1 = ctx.enter_context(tc.psum_pool(name="ps1", bufs=1))
+        pst = ctx.enter_context(tc.psum_pool(name="pst", bufs=3))
         ps2 = ctx.enter_context(tc.psum_pool(name="ps2", bufs=4))
-        if PIN:
-            ctx.enter_context(tc.manual_schedule())
+        ctx.enter_context(tc.manual_schedule())
 
-        sup_sb = const.tile([P, T * N], BF16)
-        nc.sync.dma_start(out=sup_sb[:], in_=support.rearrange("(p t) j -> p (t j)", t=T))
         x_sb = {}
 
         def load_x(m, c):
@@ -51,10 +54,17 @@ def tile_dgcn_pb_t_kernel(tc, x0, x1, x2, support, weights, biases, out):
             )
             x_sb[(m, c)] = xt
 
+        sup_sb = const.tile([P, T * N], BF16)
         w_sb = const.tile([P, M * O], BF16)
         bias_rows = const.tile([P, O], BF16)
+        ones_b = const.tile([P, P], BF16)
         nc.vector.memset(bias_rows[:], 0.0)
-        for c in range(len(CHUNKS)):
+        nc.vector.memset(ones_b[:], 1.0)
+        load_x(2, 0)
+        nc.sync.dma_start(out=sup_sb[:], in_=support.rearrange("(p t) j -> p (t j)", t=T))
+        load_x(1, 0)
+        load_x(0, 0)
+        for c in range(1, len(CHUNKS)):
             load_x(2, c)
             load_x(1, c)
             load_x(0, c)
@@ -66,14 +76,39 @@ def tile_dgcn_pb_t_kernel(tc, x0, x1, x2, support, weights, biases, out):
         make_identity(nc, ident_f[:])
         ident_b = const.tile([P, P], BF16)
         make_identity(nc, ident_b[:])
-        ones_b = const.tile([P, P], BF16)
-        nc.vector.memset(ones_b[:], 1.0)
 
+        x2g_t = {}
+        x2q_t = {}
+
+        def regroup_x2(b):
+            c, bi = chunk_of[b]
+            x2g = work.tile([P, D, T], BF16, name="x2g", tag="x2g", align_bytes=64)
+            src = x_sb[(2, c)][:, bi, :].rearrange("p (t d) -> p d t", t=T)
+            if b < HEAD_B:
+                nc.vector.tensor_copy(out=x2g[:], in_=src)
+            else:
+                nc.gpsimd.tensor_scalar(
+                    out=x2g[:], in0=src, scalar1=1.0, scalar2=0.0, op0=ALU.mult, op1=ALU.add
+                )
+            x2g_t[b] = x2g
+
+        def quantise_x2(b):
+            codes = const.tile([P, D], U32, name="x2c_%d" % b, align_bytes=64)
+            scales = const.tile([P, D], U8, name="x2s_%d" % b, align_bytes=64)
+            nc.vector.quantize_mx(
+                out=codes[:].bitcast(FP8X4),
+                scales=scales[:],
+                in_=x2g_t[b][:].rearrange("p d t -> p (d t)"),
+            )
+            x2q_t[b] = (codes, scales)
+
+        regroup_x2(0)
         sg = const.tile([P, N * 4], BF16, align_bytes=64)
         s_codes = const.tile([P, N], U32, align_bytes=64)
         s_scales = const.tile([P, N], U8, align_bytes=64)
         sup_w = sup_sb[:].bitcast(F32).rearrange("p (t i u) -> p t u i", t=T, u=2)
         sg_w = sg[:].bitcast(F32).rearrange("p (c u) -> p c u", u=2)
+        quantise_x2(0)
         for h in range(2):
             sps = ps2.tile([P, 2, 2 * P], F32, name="sps", tag="acc2")
             for tt in range(2):
@@ -87,43 +122,25 @@ def tile_dgcn_pb_t_kernel(tc, x0, x1, x2, support, weights, biases, out):
                 nc.vector.tensor_copy(out=dst, in_=src)
             else:
                 nc.scalar.copy(out=dst, in_=src)
+        regroup_x2(1)
         nc.vector.quantize_mx(out=s_codes[:].bitcast(FP8X4), scales=s_scales[:], in_=sg[:])
-
-        x2c = {}
-        x2s = {}
-
-        def prepare_x2(c):
-            b0, nb = CHUNKS[c]
-            x2g = const.tile([P, nb, D, T], BF16, name="x2g_c%d" % c, align_bytes=64)
-            nc.gpsimd.tensor_scalar(
-                out=x2g[:],
-                in0=x_sb[(2, c)][:].rearrange("p b (t d) -> p b d t", t=T),
-                scalar1=1.0,
-                scalar2=0.0,
-                op0=ALU.mult,
-                op1=ALU.add,
-            )
-            codes = const.tile([P, nb * D], U32, name="x2c_c%d" % c, align_bytes=64)
-            scales = const.tile([P, nb * D], U8, name="x2s_c%d" % c, align_bytes=64)
-            nc.vector.quantize_mx(
-                out=codes[:].bitcast(FP8X4),
-                scales=scales[:],
-                in_=x2g[:].rearrange("p b d t -> p (b d t)"),
-            )
-            x2c[c] = codes
-            x2s[c] = scales
+        quantise_x2(1)
 
         wg = const.tile([P, O * M], BF16, align_bytes=64)
         w_codes = const.tile([P, O], U32, align_bytes=64)
         w_scales = const.tile([P, O], U8, align_bytes=64)
         bias_sb = const.tile([P, O], F32)
 
-        def prepare_weights():
+        def regroup_weights():
             nc.vector.tensor_copy(
                 out=wg[:].rearrange("p (o j) -> p o j", j=M),
                 in_=w_sb[:].rearrange("p (j o) -> p o j", j=M),
             )
+
+        def quantise_weights():
             nc.vector.quantize_mx(out=w_codes[:].bitcast(FP8X4), scales=w_scales[:], in_=wg[:])
+
+        def spread_bias():
             bps = ps2.tile([P, O], F32, name="bps", tag="acc2")
             nc.tensor.matmul(bps[:], lhsT=ones_b[:], rhs=bias_rows[:], start=True, stop=True)
             nc.scalar.copy(out=bias_sb[:], in_=bps[:])
@@ -134,14 +151,15 @@ def tile_dgcn_pb_t_kernel(tc, x0, x1, x2, support, weights, biases, out):
 
         def stage1(b):
             c, bi = chunk_of[b]
+            codes, scales = x2q_t[b]
             acc1 = ps1.tile([P, T * D], F32, name="acc1", tag="acc1")
             for t in range(T):
                 nc.tensor.matmul_mx(
                     out=acc1[:, t * D : (t + 1) * D],
                     lhsT=s_codes[:, t * P : (t + 1) * P].bitcast(FP8X4),
                     lhsT_scale=s_scales[:, t * P : (t + 1) * P],
-                    rhs=x2c[c][:, bi * D : (bi + 1) * D].bitcast(FP8X4),
-                    rhs_scale=x2s[c][:, bi * D : (bi + 1) * D],
+                    rhs=codes[:].bitcast(FP8X4),
+                    rhs_scale=scales[:],
                     start=True,
                     stop=True,
                 )
@@ -169,9 +187,11 @@ def tile_dgcn_pb_t_kernel(tc, x0, x1, x2, support, weights, biases, out):
                         else:
                             src = x3_t[b][:, t * D : (t + 1) * D]
                         nc.tensor.transpose(tp[:, m, tt * P : (tt + 1) * P], src, ident_b[:])
-                nc.scalar.copy(
-                    out=xg[:, h * 2 * P : (h + 1) * 2 * P, :], in_=tp[:].rearrange("p m c -> p c m")
-                )
+                dst = xg[:, h * 2 * P : (h + 1) * 2 * P, :]
+                if f_on_vector(b, h):
+                    nc.vector.tensor_copy(out=dst, in_=tp[:].rearrange("p m c -> p c m"))
+                else:
+                    nc.scalar.copy(out=dst, in_=tp[:].rearrange("p m c -> p c m"))
             xg_t[b] = xg
 
         def quantise_x(b):
@@ -182,46 +202,61 @@ def tile_dgcn_pb_t_kernel(tc, x0, x1, x2, support, weights, biases, out):
             )
             xq_t[b] = (xc, xsc)
 
-        def stage2(b):
-            xc, xsc = xq_t[b]
-            gp_banks = GP_ODD if b % 2 else GP_EVEN
-            accs = []
-            for t in range(T):
-                acc2 = ps2.tile([P, O], F32, name="acc2", tag="acc2")
-                nc.tensor.matmul_mx(
-                    out=acc2[:],
-                    lhsT=xc[:, t * P : (t + 1) * P].bitcast(FP8X4),
-                    lhsT_scale=xsc[:, t * P : (t + 1) * P],
-                    rhs=w_codes[:].bitcast(FP8X4),
-                    rhs_scale=w_scales[:],
-                    start=True,
-                    stop=True,
-                )
-                accs.append(acc2)
-            res = outp.tile([P, T, O], F32, name="res", tag="res")
-            for t in range(T):
-                if t in gp_banks:
+        for i in range(-3, B):
+            if i >= 0:
+                xc, xsc = xq_t[i]
+                accs = []
+                for t in range(T):
+                    acc2 = ps2.tile([P, O], F32, name="acc2", tag="acc2")
+                    nc.tensor.matmul_mx(
+                        out=acc2[:],
+                        lhsT=xc[:, t * P : (t + 1) * P].bitcast(FP8X4),
+                        lhsT_scale=xsc[:, t * P : (t + 1) * P],
+                        rhs=w_codes[:].bitcast(FP8X4),
+                        rhs_scale=w_scales[:],
+                        start=True,
+                        stop=True,
+                    )
+                    accs.append(acc2)
+                res = outp.tile([P, T, O], F32, name="res", tag="res")
+                out_b = out[i].rearrange("(p t) o -> p t o", t=T)
+                last = i == B - 1
+                v_banks = [t for t in range(T) if t not in gp_banks(i)]
+                for t in gp_banks(i):
                     tmp = work.tile([P, O], F32, name="tmp", tag="tmp")
                     nc.scalar.copy(out=tmp[:], in_=accs[t][:])
                     nc.gpsimd.tensor_tensor(out=res[:, t, :], in0=tmp[:], in1=bias_sb[:], op=ALU.add)
-                else:
+                t = v_banks[0]
+                nc.vector.tensor_tensor(out=res[:, t, :], in0=accs[t][:], in1=bias_sb[:], op=ALU.add)
+                if last:
+                    nc.sync.dma_start(out=out_b[:, t, :], in_=res[:, t, :])
+            if 0 <= i + 1 < B:
+                quantise_x(i + 1)
+            if HEAD_B <= i + 4 < B:
+                quantise_x2(i + 4)
+            if i >= 0:
+                for t in v_banks[1:]:
                     nc.vector.tensor_tensor(out=res[:, t, :], in0=accs[t][:], in1=bias_sb[:], op=ALU.add)
-            nc.sync.dma_start(out=out[b].rearrange("(p t) o -> p t o", t=T), in_=res[:])
-
-        prepare_x2(0)
-        prepare_x2(1)
-        next_chunk = 2
-        for i in range(B + 3):
-            if next_chunk < len(CHUNKS) and CHUNKS[next_chunk][0] <= i + 3:
-                prepare_x2(next_chunk)
-                next_chunk += 1
-            if i == 1:
-                prepare_weights()
-            if i < B:
-                stage1(i)
-            if 0 <= i - 1 < B:
-                transposes(i - 1)
-            if 0 <= i - 2 < B:
-                quantise_x(i - 2)
-            if 0 <= i - 3 < B:
-                stage2(i - 3)
+                    if last:
+                        nc.sync.dma_start(out=out_b[:, t, :], in_=res[:, t, :])
+                if last:
+                    for t in gp_banks(i):
+                        nc.sync.dma_start(out=out_b[:, t, :], in_=res[:, t, :])
+                else:
+                    nc.sync.dma_start(out=out_b, in_=res[:])
+            if 0 <= i + 2 < B:
+                transposes(i + 2)
+            if i + 3 < B:
+                stage1(i + 3)
+            if HEAD_B <= i + 5 < B:
+                regroup_x2(i + 5)
+            if i == -3:
+                regroup_x2(2)
+                regroup_x2(3)
+                quantise_x2(2)
+                quantise_x2(3)
+            if i == -2:
+                regroup_weights()
+            if i == -1:
+                quantise_weights()
+                spread_bias()

@@ -16,15 +16,10 @@ T = N // P
 FLOPS = 2 * B * N * N * D + 2 * B * N * (D * M) * O
 
 CHUNKS = [(0, 1), (1, 1), (2, 2), (4, 4), (8, 4), (12, 4)]
-HEAD_B = 4
-
-
-def gp_banks(b):
-    return (0,)
-
-
-def f_on_vector(b, h):
-    return b < 2 and h == 0
+V_REGROUPS = 4
+RING_FROM = 6
+GP_BANK = 0
+SPLIT_FROM = 14
 
 
 def tile_dgcn_pb_t_kernel(tc, x0, x1, x2, support, weights, biases, out):
@@ -39,8 +34,8 @@ def tile_dgcn_pb_t_kernel(tc, x0, x1, x2, support, weights, biases, out):
         const = ctx.enter_context(tc.tile_pool(name="const", bufs=1))
         work = ctx.enter_context(tc.tile_pool(name="work", bufs=3))
         outp = ctx.enter_context(tc.tile_pool(name="outp", bufs=4))
-        ps1 = ctx.enter_context(tc.psum_pool(name="ps1", bufs=1))
-        pst = ctx.enter_context(tc.psum_pool(name="pst", bufs=3))
+        ps1 = ctx.enter_context(tc.psum_pool(name="ps1", bufs=2))
+        pst = ctx.enter_context(tc.psum_pool(name="pst", bufs=2))
         ps2 = ctx.enter_context(tc.psum_pool(name="ps2", bufs=4))
         ctx.enter_context(tc.manual_schedule())
 
@@ -64,13 +59,12 @@ def tile_dgcn_pb_t_kernel(tc, x0, x1, x2, support, weights, biases, out):
         nc.sync.dma_start(out=sup_sb[:], in_=support.rearrange("(p t) j -> p (t j)", t=T))
         load_x(1, 0)
         load_x(0, 0)
+        nc.sync.dma_start(out=w_sb[:], in_=weights.rearrange("(p j) o -> p (j o)", j=M))
+        nc.sync.dma_start(out=bias_rows[0:1, :], in_=biases.rearrange("(a o) -> a o", a=1))
         for c in range(1, len(CHUNKS)):
             load_x(2, c)
             load_x(1, c)
             load_x(0, c)
-            if c == 1:
-                nc.sync.dma_start(out=w_sb[:], in_=weights.rearrange("(p j) o -> p (j o)", j=M))
-                nc.sync.dma_start(out=bias_rows[0:1, :], in_=biases.rearrange("(a o) -> a o", a=1))
 
         ident_f = const.tile([P, P], F32)
         make_identity(nc, ident_f[:])
@@ -81,10 +75,15 @@ def tile_dgcn_pb_t_kernel(tc, x0, x1, x2, support, weights, biases, out):
         x2q_t = {}
 
         def regroup_x2(b):
+            if b >= B:
+                return
             c, bi = chunk_of[b]
-            x2g = work.tile([P, D, T], BF16, name="x2g", tag="x2g", align_bytes=64)
+            if b < RING_FROM:
+                x2g = const.tile([P, D, T], BF16, name="x2g_%d" % b, align_bytes=64)
+            else:
+                x2g = const.tile([P, D, T], BF16, name="x2g_ring", tag="x2g_ring", align_bytes=64)
             src = x_sb[(2, c)][:, bi, :].rearrange("p (t d) -> p d t", t=T)
-            if b < HEAD_B:
+            if b < V_REGROUPS:
                 nc.vector.tensor_copy(out=x2g[:], in_=src)
             else:
                 nc.gpsimd.tensor_scalar(
@@ -93,6 +92,8 @@ def tile_dgcn_pb_t_kernel(tc, x0, x1, x2, support, weights, biases, out):
             x2g_t[b] = x2g
 
         def quantise_x2(b):
+            if b >= B:
+                return
             codes = const.tile([P, D], U32, name="x2c_%d" % b, align_bytes=64)
             scales = const.tile([P, D], U8, name="x2s_%d" % b, align_bytes=64)
             nc.vector.quantize_mx(
@@ -102,54 +103,20 @@ def tile_dgcn_pb_t_kernel(tc, x0, x1, x2, support, weights, biases, out):
             )
             x2q_t[b] = (codes, scales)
 
-        regroup_x2(0)
         sg = const.tile([P, N * 4], BF16, align_bytes=64)
         s_codes = const.tile([P, N], U32, align_bytes=64)
         s_scales = const.tile([P, N], U8, align_bytes=64)
-        sup_w = sup_sb[:].bitcast(F32).rearrange("p (t i u) -> p t u i", t=T, u=2)
-        sg_w = sg[:].bitcast(F32).rearrange("p (c u) -> p c u", u=2)
-        quantise_x2(0)
-        for h in range(2):
-            sps = ps2.tile([P, 2, 2 * P], F32, name="sps", tag="acc2")
-            for tt in range(2):
-                for u in range(2):
-                    nc.tensor.transpose(
-                        sps[:, u, tt * P : (tt + 1) * P], sup_w[:, 2 * h + tt, u, :], ident_f[:]
-                    )
-            src = sps[:].rearrange("p u c -> p c u")
-            dst = sg_w[:, h * 2 * P : (h + 1) * 2 * P, :]
-            if h == 0:
-                nc.vector.tensor_copy(out=dst, in_=src)
-            else:
-                nc.scalar.copy(out=dst, in_=src)
-        regroup_x2(1)
-        nc.vector.quantize_mx(out=s_codes[:].bitcast(FP8X4), scales=s_scales[:], in_=sg[:])
-        quantise_x2(1)
-
         wg = const.tile([P, O * M], BF16, align_bytes=64)
         w_codes = const.tile([P, O], U32, align_bytes=64)
         w_scales = const.tile([P, O], U8, align_bytes=64)
         bias_sb = const.tile([P, O], F32)
-
-        def regroup_weights():
-            nc.vector.tensor_copy(
-                out=wg[:].rearrange("p (o j) -> p o j", j=M),
-                in_=w_sb[:].rearrange("p (j o) -> p o j", j=M),
-            )
-
-        def quantise_weights():
-            nc.vector.quantize_mx(out=w_codes[:].bitcast(FP8X4), scales=w_scales[:], in_=wg[:])
-
-        def spread_bias():
-            bps = ps2.tile([P, O], F32, name="bps", tag="acc2")
-            nc.tensor.matmul(bps[:], lhsT=ones_b[:], rhs=bias_rows[:], start=True, stop=True)
-            nc.scalar.copy(out=bias_sb[:], in_=bps[:])
-
         x3_t = {}
         xg_t = {}
         xq_t = {}
 
         def stage1(b):
+            if b >= B:
+                return
             c, bi = chunk_of[b]
             codes, scales = x2q_t[b]
             acc1 = ps1.tile([P, T * D], F32, name="acc1", tag="acc1")
@@ -175,6 +142,8 @@ def tile_dgcn_pb_t_kernel(tc, x0, x1, x2, support, weights, biases, out):
             x3_t[b] = x3
 
         def transposes(b):
+            if b >= B:
+                return
             c, bi = chunk_of[b]
             xg = work.tile([P, N, M], BF16, name="xg", tag="xg", align_bytes=64)
             for h in range(2):
@@ -187,14 +156,14 @@ def tile_dgcn_pb_t_kernel(tc, x0, x1, x2, support, weights, biases, out):
                         else:
                             src = x3_t[b][:, t * D : (t + 1) * D]
                         nc.tensor.transpose(tp[:, m, tt * P : (tt + 1) * P], src, ident_b[:])
-                dst = xg[:, h * 2 * P : (h + 1) * 2 * P, :]
-                if f_on_vector(b, h):
-                    nc.vector.tensor_copy(out=dst, in_=tp[:].rearrange("p m c -> p c m"))
-                else:
-                    nc.scalar.copy(out=dst, in_=tp[:].rearrange("p m c -> p c m"))
+                nc.scalar.copy(
+                    out=xg[:, h * 2 * P : (h + 1) * 2 * P, :], in_=tp[:].rearrange("p m c -> p c m")
+                )
             xg_t[b] = xg
 
         def quantise_x(b):
+            if b >= B:
+                return
             xc = work.tile([P, N], U32, name="xc", tag="xc", align_bytes=64)
             xsc = work.tile([P, N], U8, name="xsc", tag="xsc", align_bytes=64)
             nc.vector.quantize_mx(
@@ -202,61 +171,90 @@ def tile_dgcn_pb_t_kernel(tc, x0, x1, x2, support, weights, biases, out):
             )
             xq_t[b] = (xc, xsc)
 
-        for i in range(-3, B):
-            if i >= 0:
-                xc, xsc = xq_t[i]
-                accs = []
-                for t in range(T):
-                    acc2 = ps2.tile([P, O], F32, name="acc2", tag="acc2")
-                    nc.tensor.matmul_mx(
-                        out=acc2[:],
-                        lhsT=xc[:, t * P : (t + 1) * P].bitcast(FP8X4),
-                        lhsT_scale=xsc[:, t * P : (t + 1) * P],
-                        rhs=w_codes[:].bitcast(FP8X4),
-                        rhs_scale=w_scales[:],
-                        start=True,
-                        stop=True,
-                    )
-                    accs.append(acc2)
-                res = outp.tile([P, T, O], F32, name="res", tag="res")
-                out_b = out[i].rearrange("(p t) o -> p t o", t=T)
-                last = i == B - 1
-                v_banks = [t for t in range(T) if t not in gp_banks(i)]
-                for t in gp_banks(i):
-                    tmp = work.tile([P, O], F32, name="tmp", tag="tmp")
-                    nc.scalar.copy(out=tmp[:], in_=accs[t][:])
-                    nc.gpsimd.tensor_tensor(out=res[:, t, :], in0=tmp[:], in1=bias_sb[:], op=ALU.add)
-                t = v_banks[0]
-                nc.vector.tensor_tensor(out=res[:, t, :], in0=accs[t][:], in1=bias_sb[:], op=ALU.add)
-                if last:
-                    nc.sync.dma_start(out=out_b[:, t, :], in_=res[:, t, :])
-            if 0 <= i + 1 < B:
-                quantise_x(i + 1)
-            if HEAD_B <= i + 4 < B:
-                quantise_x2(i + 4)
-            if i >= 0:
-                for t in v_banks[1:]:
+        def stage2(b):
+            xc, xsc = xq_t[b]
+            accs = []
+            for t in range(T):
+                acc2 = ps2.tile([P, O], F32, name="acc2", tag="acc2")
+                nc.tensor.matmul_mx(
+                    out=acc2[:],
+                    lhsT=xc[:, t * P : (t + 1) * P].bitcast(FP8X4),
+                    lhsT_scale=xsc[:, t * P : (t + 1) * P],
+                    rhs=w_codes[:].bitcast(FP8X4),
+                    rhs_scale=w_scales[:],
+                    start=True,
+                    stop=True,
+                )
+                accs.append(acc2)
+            res = outp.tile([P, T, O], F32, name="res", tag="res")
+            out_b = out[b].rearrange("(p t) o -> p t o", t=T)
+            tmp = work.tile([P, O], F32, name="tmp", tag="tmp")
+            nc.scalar.copy(out=tmp[:], in_=accs[GP_BANK][:])
+            nc.gpsimd.tensor_tensor(out=res[:, GP_BANK, :], in0=tmp[:], in1=bias_sb[:], op=ALU.add)
+            for t in range(T):
+                if t != GP_BANK:
                     nc.vector.tensor_tensor(out=res[:, t, :], in0=accs[t][:], in1=bias_sb[:], op=ALU.add)
-                    if last:
+                    if b >= SPLIT_FROM:
                         nc.sync.dma_start(out=out_b[:, t, :], in_=res[:, t, :])
-                if last:
-                    for t in gp_banks(i):
-                        nc.sync.dma_start(out=out_b[:, t, :], in_=res[:, t, :])
-                else:
-                    nc.sync.dma_start(out=out_b, in_=res[:])
-            if 0 <= i + 2 < B:
-                transposes(i + 2)
-            if i + 3 < B:
-                stage1(i + 3)
-            if HEAD_B <= i + 5 < B:
-                regroup_x2(i + 5)
-            if i == -3:
-                regroup_x2(2)
-                regroup_x2(3)
-                quantise_x2(2)
-                quantise_x2(3)
-            if i == -2:
-                regroup_weights()
-            if i == -1:
-                quantise_weights()
-                spread_bias()
+            if b >= SPLIT_FROM:
+                nc.sync.dma_start(out=out_b[:, GP_BANK, :], in_=res[:, GP_BANK, :])
+            else:
+                nc.sync.dma_start(out=out_b, in_=res[:])
+
+        regroup_x2(0)
+        quantise_x2(0)
+        sup_w = sup_sb[:].bitcast(F32).rearrange("p (t i u) -> p t u i", t=T, u=2)
+        sg_w = sg[:].bitcast(F32).rearrange("p (c u) -> p c u", u=2)
+        for h in range(2):
+            sps = ps2.tile([P, 2, 2 * P], F32, name="sps", tag="acc2")
+            for tt in range(2):
+                for u in range(2):
+                    nc.tensor.transpose(
+                        sps[:, u, tt * P : (tt + 1) * P], sup_w[:, 2 * h + tt, u, :], ident_f[:]
+                    )
+            src = sps[:].rearrange("p u c -> p c u")
+            dst = sg_w[:, h * 2 * P : (h + 1) * 2 * P, :]
+            if h == 0:
+                nc.vector.tensor_copy(out=dst, in_=src)
+            else:
+                nc.scalar.copy(out=dst, in_=src)
+        bps = ps2.tile([P, O], F32, name="bps", tag="acc2")
+        nc.tensor.matmul(bps[:], lhsT=ones_b[:], rhs=bias_rows[:], start=True, stop=True)
+        nc.scalar.copy(
+            out=wg[:].rearrange("p (o j) -> p o j", j=M), in_=w_sb[:].rearrange("p (j o) -> p o j", j=M)
+        )
+        nc.scalar.copy(out=bias_sb[:], in_=bps[:])
+        nc.vector.quantize_mx(out=s_codes[:].bitcast(FP8X4), scales=s_scales[:], in_=sg[:])
+        regroup_x2(1)
+        quantise_x2(1)
+        stage1(0)
+        stage1(1)
+        regroup_x2(2)
+        quantise_x2(2)
+        transposes(0)
+        nc.vector.quantize_mx(out=w_codes[:].bitcast(FP8X4), scales=w_scales[:], in_=wg[:])
+        stage1(2)
+        regroup_x2(3)
+        quantise_x2(3)
+        transposes(1)
+        quantise_x(0)
+        stage1(3)
+        regroup_x2(4)
+        stage2(0)
+        transposes(2)
+        quantise_x(1)
+        quantise_x2(4)
+        regroup_x2(5)
+        quantise_x(2)
+        quantise_x2(5)
+        transposes(3)
+        stage1(4)
+        regroup_x2(6)
+
+        for i in range(1, B):
+            stage2(i)
+            quantise_x(i + 2)
+            quantise_x2(i + 5)
+            transposes(i + 3)
+            stage1(i + 4)
+            regroup_x2(i + 6)

@@ -19,7 +19,7 @@ CHUNKS = [(0, 1), (1, 1), (2, 2), (4, 4), (8, 4), (12, 4)]
 V_REGROUPS = 4
 RING_FROM = 6
 GP_BANK = 0
-SPLIT_FROM = 14
+SPLIT_FROM = 12
 
 
 def tile_dgcn_pb_t_kernel(tc, x0, x1, x2, support, weights, biases, out):
@@ -55,6 +55,15 @@ def tile_dgcn_pb_t_kernel(tc, x0, x1, x2, support, weights, biases, out):
         ones_b = const.tile([P, P], BF16)
         nc.vector.memset(bias_rows[:], 0.0)
         nc.vector.memset(ones_b[:], 1.0)
+        warm_rhs = const.tile([P, O], BF16)
+        nc.vector.memset(warm_rhs[:], 0.0)
+
+        def warm(n):
+            dum = ps2.tile([P, O], F32, name="dum", tag="acc2")
+            for k in range(n):
+                nc.tensor.matmul(dum[:], lhsT=ones_b[:], rhs=warm_rhs[:], start=True, stop=True)
+
+        warm(7)
         load_x(2, 0)
         nc.sync.dma_start(out=sup_sb[:], in_=support.rearrange("(p t) j -> p (t j)", t=T))
         load_x(1, 0)
@@ -218,6 +227,7 @@ def tile_dgcn_pb_t_kernel(tc, x0, x1, x2, support, weights, biases, out):
                 nc.vector.tensor_copy(out=dst, in_=src)
             else:
                 nc.scalar.copy(out=dst, in_=src)
+        warm(4)
         bps = ps2.tile([P, O], F32, name="bps", tag="acc2")
         nc.tensor.matmul(bps[:], lhsT=ones_b[:], rhs=bias_rows[:], start=True, stop=True)
         nc.scalar.copy(
@@ -229,11 +239,13 @@ def tile_dgcn_pb_t_kernel(tc, x0, x1, x2, support, weights, biases, out):
         quantise_x2(1)
         stage1(0)
         stage1(1)
+        warm(2)
         regroup_x2(2)
         quantise_x2(2)
         transposes(0)
         nc.vector.quantize_mx(out=w_codes[:].bitcast(FP8X4), scales=w_scales[:], in_=wg[:])
         stage1(2)
+        warm(2)
         regroup_x2(3)
         quantise_x2(3)
         transposes(1)

@@ -13,13 +13,17 @@ ALU = mybir.AluOpType
 P = 128
 B, N, D, O, M = 16, 512, 128, 512, 4
 T = N // P
+H = 2
+W2 = 2 * P
 FLOPS = 2 * B * N * N * D + 2 * B * N * (D * M) * O
 
 CHUNKS = [(0, 1), (1, 1), (2, 2), (4, 4), (8, 4), (12, 4)]
-V_REGROUPS = 4
-RING_FROM = 6
-GP_BANK = 0
 SPLIT_FROM = 12
+GP1 = (0,)
+GP2 = (0, 2)
+TWO = ()
+V_REGROUPS = 2
+RING_FROM = 3
 
 
 def tile_dgcn_pb_t_kernel(tc, x0, x1, x2, support, weights, biases, out):
@@ -33,7 +37,7 @@ def tile_dgcn_pb_t_kernel(tc, x0, x1, x2, support, weights, biases, out):
     with ExitStack() as ctx:
         const = ctx.enter_context(tc.tile_pool(name="const", bufs=1))
         work = ctx.enter_context(tc.tile_pool(name="work", bufs=3))
-        outp = ctx.enter_context(tc.tile_pool(name="outp", bufs=4))
+        outp = ctx.enter_context(tc.tile_pool(name="outp", bufs=5))
         ps1 = ctx.enter_context(tc.psum_pool(name="ps1", bufs=2))
         pst = ctx.enter_context(tc.psum_pool(name="pst", bufs=2))
         ps2 = ctx.enter_context(tc.psum_pool(name="ps2", bufs=4))
@@ -49,28 +53,38 @@ def tile_dgcn_pb_t_kernel(tc, x0, x1, x2, support, weights, biases, out):
             )
             x_sb[(m, c)] = xt
 
-        sup_sb = const.tile([P, T * N], BF16)
-        w_sb = const.tile([P, M * O], BF16)
+        sup_sb = []
         bias_rows = const.tile([P, O], BF16)
         ones_b = const.tile([P, P], BF16)
-        nc.vector.memset(bias_rows[:], 0.0)
-        nc.vector.memset(ones_b[:], 1.0)
         warm_rhs = const.tile([P, O], BF16)
+        nc.vector.memset(ones_b[:], 1.0)
         nc.vector.memset(warm_rhs[:], 0.0)
+        nc.vector.memset(bias_rows[:], 0.0)
 
         def warm(n):
             dum = ps2.tile([P, O], F32, name="dum", tag="acc2")
             for k in range(n):
                 nc.tensor.matmul(dum[:], lhsT=ones_b[:], rhs=warm_rhs[:], start=True, stop=True)
 
-        warm(7)
+        warm(6)
         load_x(2, 0)
-        nc.sync.dma_start(out=sup_sb[:], in_=support.rearrange("(p t) j -> p (t j)", t=T))
+        sup_view = support.rearrange("(p t) j -> p t j", t=T)
+        for h in range(H):
+            s_half = const.tile([P, 2, N], BF16, name="sup%d" % h)
+            nc.sync.dma_start(out=s_half[:], in_=sup_view[:, 2 * h : 2 * h + 2, :])
+            sup_sb.append(s_half)
+        w_sb = const.tile([P, M * O], BF16)
+        nc.sync.dma_start(out=bias_rows[0:1, :], in_=biases.rearrange("(a o) -> a o", a=1))
+        nc.sync.dma_start(out=w_sb[:], in_=weights.rearrange("(p j) o -> p (j o)", j=M))
         load_x(1, 0)
         load_x(0, 0)
-        nc.sync.dma_start(out=w_sb[:], in_=weights.rearrange("(p j) o -> p (j o)", j=M))
-        nc.sync.dma_start(out=bias_rows[0:1, :], in_=biases.rearrange("(a o) -> a o", a=1))
-        for c in range(1, len(CHUNKS)):
+        load_x(2, 1)
+        load_x(2, 2)
+        load_x(1, 1)
+        load_x(0, 1)
+        load_x(1, 2)
+        load_x(0, 2)
+        for c in range(3, len(CHUNKS)):
             load_x(2, c)
             load_x(1, c)
             load_x(0, c)
@@ -78,7 +92,7 @@ def tile_dgcn_pb_t_kernel(tc, x0, x1, x2, support, weights, biases, out):
         ident_f = const.tile([P, P], F32)
         make_identity(nc, ident_f[:])
         ident_b = const.tile([P, P], BF16)
-        make_identity(nc, ident_b[:])
+        nc.vector.tensor_copy(out=ident_b[:], in_=ident_f[:])
 
         x2g_t = {}
         x2q_t = {}
@@ -95,9 +109,7 @@ def tile_dgcn_pb_t_kernel(tc, x0, x1, x2, support, weights, biases, out):
             if b < V_REGROUPS:
                 nc.vector.tensor_copy(out=x2g[:], in_=src)
             else:
-                nc.gpsimd.tensor_scalar(
-                    out=x2g[:], in0=src, scalar1=1.0, scalar2=0.0, op0=ALU.mult, op1=ALU.add
-                )
+                nc.gpsimd.tensor_scalar(out=x2g[:], in0=src, scalar1=1.0, scalar2=0.0, op0=ALU.mult, op1=ALU.add)
             x2g_t[b] = x2g
 
         def quantise_x2(b):
@@ -105,11 +117,7 @@ def tile_dgcn_pb_t_kernel(tc, x0, x1, x2, support, weights, biases, out):
                 return
             codes = const.tile([P, D], U32, name="x2c_%d" % b, align_bytes=64)
             scales = const.tile([P, D], U8, name="x2s_%d" % b, align_bytes=64)
-            nc.vector.quantize_mx(
-                out=codes[:].bitcast(FP8X4),
-                scales=scales[:],
-                in_=x2g_t[b][:].rearrange("p d t -> p (d t)"),
-            )
+            nc.vector.quantize_mx(out=codes[:].bitcast(FP8X4), scales=scales[:], in_=x2g_t[b][:].rearrange("p d t -> p (d t)"))
             x2q_t[b] = (codes, scales)
 
         sg = const.tile([P, N * 4], BF16, align_bytes=64)
@@ -120,18 +128,21 @@ def tile_dgcn_pb_t_kernel(tc, x0, x1, x2, support, weights, biases, out):
         w_scales = const.tile([P, O], U8, align_bytes=64)
         bias_sb = const.tile([P, O], F32)
         x3_t = {}
+        acc1_t = {}
         xg_t = {}
         xq_t = {}
+        tp_t = {}
 
-        def stage1(b):
+        def stage1(b, tiles=range(T)):
             if b >= B:
                 return
-            c, bi = chunk_of[b]
             codes, scales = x2q_t[b]
-            acc1 = ps1.tile([P, T * D], F32, name="acc1", tag="acc1")
-            for t in range(T):
+            if b not in acc1_t:
+                acc1 = ps1.tile([P, T * D], F32, name="acc1", tag="acc1")
+                acc1_t[b] = acc1
+            for t in tiles:
                 nc.tensor.matmul_mx(
-                    out=acc1[:, t * D : (t + 1) * D],
+                    out=acc1_t[b][:, t * D : (t + 1) * D],
                     lhsT=s_codes[:, t * P : (t + 1) * P].bitcast(FP8X4),
                     lhsT_scale=s_scales[:, t * P : (t + 1) * P],
                     rhs=codes[:].bitcast(FP8X4),
@@ -139,51 +150,61 @@ def tile_dgcn_pb_t_kernel(tc, x0, x1, x2, support, weights, biases, out):
                     start=True,
                     stop=True,
                 )
-            x3 = work.tile([P, T * D], BF16, name="x3", tag="x3")
-            nc.vector.scalar_tensor_tensor(
-                out=x3[:],
-                in0=acc1[:],
-                scalar=2.0,
-                in1=x_sb[(1, c)][:, bi, :],
-                op0=ALU.mult,
-                op1=ALU.subtract,
-            )
-            x3_t[b] = x3
 
-        def transposes(b):
+        def order3(b, lo=0, hi=T * D):
             if b >= B:
                 return
             c, bi = chunk_of[b]
-            xg = work.tile([P, N, M], BF16, name="xg", tag="xg", align_bytes=64)
-            for h in range(2):
-                tp = pst.tile([P, M, 2 * P], BF16, name="tp", tag="tp")
-                for m in range(M):
-                    for tt in range(2):
-                        t = 2 * h + tt
-                        if m < 3:
-                            src = x_sb[(m, c)][:, bi, t * D : (t + 1) * D]
-                        else:
-                            src = x3_t[b][:, t * D : (t + 1) * D]
-                        nc.tensor.transpose(tp[:, m, tt * P : (tt + 1) * P], src, ident_b[:])
-                nc.scalar.copy(
-                    out=xg[:, h * 2 * P : (h + 1) * 2 * P, :], in_=tp[:].rearrange("p m c -> p c m")
-                )
-            xg_t[b] = xg
+            if b not in x3_t:
+                x3 = work.tile([P, T * D], BF16, name="x3", tag="x3")
+                x3_t[b] = x3
+            nc.vector.scalar_tensor_tensor(
+                out=x3_t[b][:, lo:hi], in0=acc1_t[b][:, lo:hi], scalar=2.0, in1=x_sb[(1, c)][:, bi, lo:hi],
+                op0=ALU.mult, op1=ALU.subtract,
+            )
 
-        def quantise_x(b):
+        def transposes(b, orders=(0, 1, 2, 3), halves=(0, 1)):
             if b >= B:
                 return
-            xc = work.tile([P, N], U32, name="xc", tag="xc", align_bytes=64)
-            xsc = work.tile([P, N], U8, name="xsc", tag="xsc", align_bytes=64)
-            nc.vector.quantize_mx(
-                out=xc[:].bitcast(FP8X4), scales=xsc[:], in_=xg_t[b][:].rearrange("p c m -> p (c m)")
-            )
-            xq_t[b] = (xc, xsc)
+            c, bi = chunk_of[b]
+            for h in halves:
+                if (b, h) not in tp_t:
+                    tp = pst.tile([P, M, W2], BF16, name="tp", tag="tp")
+                    tp_t[(b, h)] = tp
+                for m in orders:
+                    for tt in range(2):
+                        t = 2 * h + tt
+                        src = x_sb[(m, c)][:, bi, t * D : (t + 1) * D] if m < 3 else x3_t[b][:, t * D : (t + 1) * D]
+                        nc.tensor.transpose(tp_t[(b, h)][:, m, tt * P : (tt + 1) * P], src, ident_b[:])
 
-        def stage2(b):
+        def interleave(b, h, copy, lo=0, hi=W2):
+            if b >= B:
+                return
+            if b not in xg_t:
+                xg = work.tile([P, N, M], BF16, name="xg", tag="xg", align_bytes=64)
+                xg_t[b] = xg
+            copy(
+                out=xg_t[b][:, h * W2 + lo : h * W2 + hi, :],
+                in_=tp_t[(b, h)][:, :, lo:hi].rearrange("p m c -> p c m"),
+            )
+
+        def quantise_x(b, lo=0, hi=N):
+            if b >= B:
+                return
+            if b not in xq_t:
+                xc = work.tile([P, N], U32, name="xc", tag="xc", align_bytes=64)
+                xsc = work.tile([P, N], U8, name="xsc", tag="xsc", align_bytes=64)
+                xq_t[b] = (xc, xsc)
             xc, xsc = xq_t[b]
-            accs = []
-            for t in range(T):
+            nc.vector.quantize_mx(
+                out=xc[:, lo:hi].bitcast(FP8X4), scales=xsc[:, lo:hi], in_=xg_t[b][:, lo:hi, :].rearrange("p c m -> p (c m)")
+            )
+
+        acc2_t = {}
+
+        def stage2(b, tiles=range(T)):
+            xc, xsc = xq_t[b]
+            for t in tiles:
                 acc2 = ps2.tile([P, O], F32, name="acc2", tag="acc2")
                 nc.tensor.matmul_mx(
                     out=acc2[:],
@@ -194,79 +215,119 @@ def tile_dgcn_pb_t_kernel(tc, x0, x1, x2, support, weights, biases, out):
                     start=True,
                     stop=True,
                 )
-                accs.append(acc2)
+                acc2_t[(b, t)] = acc2
+
+        def finish(b):
             res = outp.tile([P, T, O], F32, name="res", tag="res")
             out_b = out[b].rearrange("(p t) o -> p t o", t=T)
-            tmp = work.tile([P, O], F32, name="tmp", tag="tmp")
-            nc.scalar.copy(out=tmp[:], in_=accs[GP_BANK][:])
-            nc.gpsimd.tensor_tensor(out=res[:, GP_BANK, :], in0=tmp[:], in1=bias_sb[:], op=ALU.add)
+            gp_banks = GP2 if b in TWO else GP1
+            for t in gp_banks:
+                tmp = work.tile([P, O], F32, name="tmp", tag="tmp")
+                nc.scalar.copy(out=tmp[:], in_=acc2_t[(b, t)][:])
+                nc.gpsimd.tensor_tensor(out=res[:, t, :], in0=tmp[:], in1=bias_sb[:], op=ALU.add)
             for t in range(T):
-                if t != GP_BANK:
-                    nc.vector.tensor_tensor(out=res[:, t, :], in0=accs[t][:], in1=bias_sb[:], op=ALU.add)
+                if t not in gp_banks:
+                    nc.vector.tensor_tensor(out=res[:, t, :], in0=acc2_t[(b, t)][:], in1=bias_sb[:], op=ALU.add)
                     if b >= SPLIT_FROM:
                         nc.sync.dma_start(out=out_b[:, t, :], in_=res[:, t, :])
             if b >= SPLIT_FROM:
-                nc.sync.dma_start(out=out_b[:, GP_BANK, :], in_=res[:, GP_BANK, :])
+                for t in gp_banks:
+                    nc.sync.dma_start(out=out_b[:, t, :], in_=res[:, t, :])
             else:
                 nc.sync.dma_start(out=out_b, in_=res[:])
 
         regroup_x2(0)
         quantise_x2(0)
-        sup_w = sup_sb[:].bitcast(F32).rearrange("p (t i u) -> p t u i", t=T, u=2)
         sg_w = sg[:].bitcast(F32).rearrange("p (c u) -> p c u", u=2)
-        for h in range(2):
-            sps = ps2.tile([P, 2, 2 * P], F32, name="sps", tag="acc2")
+        for h in range(H):
+            sup_w = sup_sb[h][:].rearrange("p t j -> p (t j)").bitcast(F32).rearrange("p (t i u) -> p t u i", t=2, u=2)
+            sps = ps2.tile([P, 2, W2], F32, name="sps", tag="acc2")
             for tt in range(2):
                 for u in range(2):
-                    nc.tensor.transpose(
-                        sps[:, u, tt * P : (tt + 1) * P], sup_w[:, 2 * h + tt, u, :], ident_f[:]
-                    )
+                    nc.tensor.transpose(sps[:, u, tt * P : (tt + 1) * P], sup_w[:, tt, u, :], ident_f[:])
             src = sps[:].rearrange("p u c -> p c u")
-            dst = sg_w[:, h * 2 * P : (h + 1) * 2 * P, :]
+            dst = sg_w[:, h * W2 : (h + 1) * W2, :]
             if h == 0:
                 nc.vector.tensor_copy(out=dst, in_=src)
             else:
                 nc.scalar.copy(out=dst, in_=src)
-        warm(4)
+        w_view = w_sb[:].rearrange("p (j o) -> p o j", j=M)
+        wg_view = wg[:].rearrange("p (o j) -> p o j", j=M)
+        Q = O // 4
+
+        def regroup_w(k, engine):
+            g = slice(k * Q, (k + 1) * Q)
+            engine(out=wg_view[:, g, :], in_=w_view[:, g, :])
+
+        def quantise_s(h):
+            nc.vector.quantize_mx(
+                out=s_codes[:, h * W2 : (h + 1) * W2].bitcast(FP8X4), scales=s_scales[:, h * W2 : (h + 1) * W2],
+                in_=sg[:, h * W2 * 4 : (h + 1) * W2 * 4],
+            )
+
+        warm(2)
         bps = ps2.tile([P, O], F32, name="bps", tag="acc2")
         nc.tensor.matmul(bps[:], lhsT=ones_b[:], rhs=bias_rows[:], start=True, stop=True)
-        nc.scalar.copy(
-            out=wg[:].rearrange("p (o j) -> p o j", j=M), in_=w_sb[:].rearrange("p (j o) -> p o j", j=M)
-        )
+        regroup_w(0, nc.scalar.copy)
+        regroup_w(1, nc.scalar.copy)
         nc.scalar.copy(out=bias_sb[:], in_=bps[:])
-        nc.vector.quantize_mx(out=s_codes[:].bitcast(FP8X4), scales=s_scales[:], in_=sg[:])
+        quantise_s(0)
+        stage1(0, (0, 1))
+        regroup_w(2, nc.vector.tensor_copy)
+        quantise_s(1)
+        order3(0, 0, W2)
+        regroup_w(3, nc.vector.tensor_copy)
+        transposes(0, (0, 1, 2), (0, 1))
+        transposes(0, (3,), (0,))
+        interleave(0, 0, nc.scalar.copy)
+        stage1(0, (2, 3))
         regroup_x2(1)
+        order3(0, W2, 2 * W2)
         quantise_x2(1)
-        stage1(0)
+        transposes(0, (3,), (1,))
+        interleave(0, 1, nc.scalar.copy)
         stage1(1)
-        warm(2)
-        regroup_x2(2)
-        quantise_x2(2)
-        transposes(0)
-        nc.vector.quantize_mx(out=w_codes[:].bitcast(FP8X4), scales=w_scales[:], in_=wg[:])
-        stage1(2)
-        warm(2)
-        regroup_x2(3)
-        quantise_x2(3)
+        quantise_x(0, 0, W2)
+        order3(1)
+        for b in range(2, 4):
+            regroup_x2(b)
         transposes(1)
-        quantise_x(0)
-        stage1(3)
-        regroup_x2(4)
+        interleave(1, 0, nc.scalar.copy)
+        interleave(1, 1, nc.scalar.copy)
+        quantise_x2(2)
+        stage1(2)
+        nc.vector.quantize_mx(out=w_codes[:].bitcast(FP8X4), scales=w_scales[:], in_=wg[:])
+        quantise_x(0, W2, N)
+        order3(2)
         stage2(0)
+        quantise_x2(3)
+        regroup_x2(4)
         transposes(2)
+        finish(0)
+        interleave(2, 0, nc.scalar.copy)
+        interleave(2, 1, nc.scalar.copy)
+        stage1(3)
         quantise_x(1)
         quantise_x2(4)
+        order3(3)
         regroup_x2(5)
+        transposes(3)
+        interleave(3, 0, nc.scalar.copy)
+        interleave(3, 1, nc.scalar.copy)
+        stage1(4)
         quantise_x(2)
         quantise_x2(5)
-        transposes(3)
-        stage1(4)
+        order3(4)
         regroup_x2(6)
 
         for i in range(1, B):
             stage2(i)
+            finish(i)
             quantise_x(i + 2)
             quantise_x2(i + 5)
             transposes(i + 3)
+            interleave(i + 3, 0, nc.scalar.copy)
+            interleave(i + 3, 1, nc.scalar.copy)
             stage1(i + 4)
+            order3(i + 4)
             regroup_x2(i + 6)

@@ -23,6 +23,8 @@ GP1 = (0,)
 GP2 = (0, 2)
 TWO = ()
 V_REGROUPS = 2
+FILL = {0: 0, 1: 512, 2: 512, 3: 512}
+FILL_LOOP = 256
 RING_FROM = 3
 
 
@@ -171,6 +173,11 @@ def tile_dgcn_pb_t_kernel(tc, x0, x1, x2, support, weights, biases, out):
                 if (b, h) not in tp_t:
                     tp = pst.tile([P, M, W2], BF16, name="tp", tag="tp")
                     tp_t[(b, h)] = tp
+                fill = FILL.get(b, FILL_LOOP)
+                if fill and 0 in orders and (h == 1 or b < 4):
+                    nc.tensor.matmul(
+                        tp_t[(b, h)][:].rearrange("p m c -> p (m c)")[:, :fill], lhsT=ones_b[:], rhs=warm_rhs[:, :fill], start=True, stop=True
+                    )
                 for m in orders:
                     for tt in range(2):
                         t = 2 * h + tt
@@ -281,12 +288,15 @@ def tile_dgcn_pb_t_kernel(tc, x0, x1, x2, support, weights, biases, out):
         transposes(0, (3,), (0,))
         interleave(0, 0, nc.scalar.copy)
         stage1(0, (2, 3))
+        warm(2)
         regroup_x2(1)
         order3(0, W2, 2 * W2)
         quantise_x2(1)
         transposes(0, (3,), (1,))
         interleave(0, 1, nc.scalar.copy)
+        warm(1)
         stage1(1)
+        warm(1)
         quantise_x(0, 0, W2)
         order3(1)
         for b in range(2, 4):
@@ -307,17 +317,17 @@ def tile_dgcn_pb_t_kernel(tc, x0, x1, x2, support, weights, biases, out):
         interleave(2, 0, nc.scalar.copy)
         interleave(2, 1, nc.scalar.copy)
         stage1(3)
-        quantise_x(1)
-        quantise_x2(4)
         order3(3)
+        quantise_x2(4)
+        quantise_x(1)
         regroup_x2(5)
         transposes(3)
         interleave(3, 0, nc.scalar.copy)
         interleave(3, 1, nc.scalar.copy)
         stage1(4)
         quantise_x(2)
-        quantise_x2(5)
         order3(4)
+        quantise_x2(5)
         regroup_x2(6)
 
         for i in range(1, B):

@@ -22,7 +22,7 @@ SPLIT_FROM = 12
 GP1 = (0,)
 GP2 = (0, 2)
 TWO = ()
-V_REGROUPS = 2
+V_REGROUPS = (0, 1, 2, 3)
 FILL = {0: 0, 1: 512, 2: 512, 3: 512}
 FILL_LOOP = 256
 RING_FROM = 3
@@ -68,13 +68,13 @@ def tile_dgcn_pb_t_kernel(tc, x0, x1, x2, support, weights, biases, out):
             for k in range(n):
                 nc.tensor.matmul(dum[:], lhsT=ones_b[:], rhs=warm_rhs[:], start=True, stop=True)
 
-        warm(6)
-        load_x(2, 0)
+        warm(4)
         sup_view = support.rearrange("(p t) j -> p t j", t=T)
         for h in range(H):
             s_half = const.tile([P, 2, N], BF16, name="sup%d" % h)
             nc.sync.dma_start(out=s_half[:], in_=sup_view[:, 2 * h : 2 * h + 2, :])
             sup_sb.append(s_half)
+        load_x(2, 0)
         w_sb = const.tile([P, M * O], BF16)
         nc.sync.dma_start(out=bias_rows[0:1, :], in_=biases.rearrange("(a o) -> a o", a=1))
         nc.sync.dma_start(out=w_sb[:], in_=weights.rearrange("(p j) o -> p (j o)", j=M))
@@ -108,7 +108,7 @@ def tile_dgcn_pb_t_kernel(tc, x0, x1, x2, support, weights, biases, out):
             else:
                 x2g = const.tile([P, D, T], BF16, name="x2g_ring", tag="x2g_ring", align_bytes=64)
             src = x_sb[(2, c)][:, bi, :].rearrange("p (t d) -> p d t", t=T)
-            if b < V_REGROUPS:
+            if b in V_REGROUPS:
                 nc.vector.tensor_copy(out=x2g[:], in_=src)
             else:
                 nc.gpsimd.tensor_scalar(out=x2g[:], in0=src, scalar1=1.0, scalar2=0.0, op0=ALU.mult, op1=ALU.add)
@@ -243,21 +243,22 @@ def tile_dgcn_pb_t_kernel(tc, x0, x1, x2, support, weights, biases, out):
             else:
                 nc.sync.dma_start(out=out_b, in_=res[:])
 
-        regroup_x2(0)
-        quantise_x2(0)
         sg_w = sg[:].bitcast(F32).rearrange("p (c u) -> p c u", u=2)
         for h in range(H):
             sup_w = sup_sb[h][:].rearrange("p t j -> p (t j)").bitcast(F32).rearrange("p (t i u) -> p t u i", t=2, u=2)
-            sps = ps2.tile([P, 2, W2], F32, name="sps", tag="acc2")
             for tt in range(2):
+                sps = ps2.tile([P, 2, P], F32, name="sps", tag="acc2")
                 for u in range(2):
-                    nc.tensor.transpose(sps[:, u, tt * P : (tt + 1) * P], sup_w[:, tt, u, :], ident_f[:])
-            src = sps[:].rearrange("p u c -> p c u")
-            dst = sg_w[:, h * W2 : (h + 1) * W2, :]
-            if h == 0:
-                nc.vector.tensor_copy(out=dst, in_=src)
-            else:
-                nc.scalar.copy(out=dst, in_=src)
+                    nc.tensor.transpose(sps[:, u, :], sup_w[:, tt, u, :], ident_f[:])
+                src = sps[:].rearrange("p u c -> p c u")
+                t = 2 * h + tt
+                dst = sg_w[:, t * P : (t + 1) * P, :]
+                if tt == 0:
+                    nc.vector.tensor_copy(out=dst, in_=src)
+                    if h == 0:
+                        regroup_x2(0)
+                else:
+                    nc.scalar.copy(out=dst, in_=src)
         w_view = w_sb[:].rearrange("p (j o) -> p o j", j=M)
         wg_view = wg[:].rearrange("p (o j) -> p o j", j=M)
         Q = O // 4
@@ -278,8 +279,10 @@ def tile_dgcn_pb_t_kernel(tc, x0, x1, x2, support, weights, biases, out):
         regroup_w(0, nc.scalar.copy)
         regroup_w(1, nc.scalar.copy)
         nc.scalar.copy(out=bias_sb[:], in_=bps[:])
+        quantise_x2(0)
         quantise_s(0)
         stage1(0, (0, 1))
+        warm(2)
         regroup_w(2, nc.vector.tensor_copy)
         quantise_s(1)
         order3(0, 0, W2)
@@ -292,6 +295,7 @@ def tile_dgcn_pb_t_kernel(tc, x0, x1, x2, support, weights, biases, out):
         regroup_x2(1)
         order3(0, W2, 2 * W2)
         quantise_x2(1)
+        nc.vector.quantize_mx(out=w_codes[:].bitcast(FP8X4), scales=w_scales[:], in_=wg[:])
         transposes(0, (3,), (1,))
         interleave(0, 1, nc.scalar.copy)
         warm(1)
@@ -306,7 +310,6 @@ def tile_dgcn_pb_t_kernel(tc, x0, x1, x2, support, weights, biases, out):
         interleave(1, 1, nc.scalar.copy)
         quantise_x2(2)
         stage1(2)
-        nc.vector.quantize_mx(out=w_codes[:].bitcast(FP8X4), scales=w_scales[:], in_=wg[:])
         quantise_x(0, W2, N)
         order3(2)
         stage2(0)
@@ -314,9 +317,9 @@ def tile_dgcn_pb_t_kernel(tc, x0, x1, x2, support, weights, biases, out):
         regroup_x2(4)
         transposes(2)
         finish(0)
+        stage1(3)
         interleave(2, 0, nc.scalar.copy)
         interleave(2, 1, nc.scalar.copy)
-        stage1(3)
         order3(3)
         quantise_x2(4)
         quantise_x(1)

@@ -24,7 +24,7 @@ GP2 = (0, 2)
 TWO = ()
 V_REGROUPS = (0, 1, 2, 3)
 FILL = {0: 0, 1: 512, 2: 512, 3: 512}
-FILL_LOOP = 256
+FILL_LOOP = 128
 RING_FROM = 3
 
 

@@ -40,8 +40,8 @@ def tile_dgcn_pb_t_kernel(tc, x0, x1, x2, support, weights, biases, out):
         const = ctx.enter_context(tc.tile_pool(name="const", bufs=1))
         work = ctx.enter_context(tc.tile_pool(name="work", bufs=3))
         outp = ctx.enter_context(tc.tile_pool(name="outp", bufs=5))
-        ps1 = ctx.enter_context(tc.psum_pool(name="ps1", bufs=2))
-        pst = ctx.enter_context(tc.psum_pool(name="pst", bufs=2))
+        ps1 = ctx.enter_context(tc.psum_pool(name="ps1", bufs=1))
+        pst = ctx.enter_context(tc.psum_pool(name="pst", bufs=3))
         ps2 = ctx.enter_context(tc.psum_pool(name="ps2", bufs=4))
         ctx.enter_context(tc.manual_schedule())
 

@@ -18,12 +18,12 @@ W2 = 2 * P
 FLOPS = 2 * B * N * N * D + 2 * B * N * (D * M) * O
 
 CHUNKS = [(0, 1), (1, 1), (2, 2), (4, 4), (8, 4), (12, 4)]
-SPLIT_FROM = 12
+SPLIT_FROM = 15
 GP1 = (0,)
 GP2 = (0, 2)
 TWO = ()
 V_REGROUPS = (0, 1, 2, 3)
-FILL = {0: 0, 1: 512, 2: 512, 3: 512}
+FILL = {(0, 0): 0, (0, 1): 0, (1, 0): 512, (1, 1): 512, (2, 0): 512, (2, 1): 0, (3, 0): 512, (3, 1): 0}
 FILL_LOOP = 128
 RING_FROM = 3
 
@@ -173,8 +173,8 @@ def tile_dgcn_pb_t_kernel(tc, x0, x1, x2, support, weights, biases, out):
                 if (b, h) not in tp_t:
                     tp = pst.tile([P, M, W2], BF16, name="tp", tag="tp")
                     tp_t[(b, h)] = tp
-                fill = FILL.get(b, FILL_LOOP)
-                if fill and 0 in orders and (h == 1 or b < 4):
+                fill = FILL.get((b, h), FILL_LOOP if h == 1 else 0)
+                if fill and 0 in orders:
                     nc.tensor.matmul(
                         tp_t[(b, h)][:].rearrange("p m c -> p (m c)")[:, :fill], lhsT=ones_b[:], rhs=warm_rhs[:, :fill], start=True, stop=True
                     )
@@ -293,12 +293,11 @@ def tile_dgcn_pb_t_kernel(tc, x0, x1, x2, support, weights, biases, out):
         stage1(0, (2, 3))
         warm(2)
         regroup_x2(1)
-        order3(0, W2, 2 * W2)
         quantise_x2(1)
+        order3(0, W2, 2 * W2)
         nc.vector.quantize_mx(out=w_codes[:].bitcast(FP8X4), scales=w_scales[:], in_=wg[:])
         transposes(0, (3,), (1,))
         interleave(0, 1, nc.scalar.copy)
-        warm(1)
         stage1(1)
         warm(1)
         quantise_x(0, 0, W2)
@@ -315,32 +314,33 @@ def tile_dgcn_pb_t_kernel(tc, x0, x1, x2, support, weights, biases, out):
         stage2(0)
         quantise_x2(3)
         regroup_x2(4)
-        transposes(2)
-        finish(0)
+        transposes(2, halves=(0,))
         stage1(3)
+        transposes(2, halves=(1,))
+        finish(0)
         interleave(2, 0, nc.scalar.copy)
         interleave(2, 1, nc.scalar.copy)
         order3(3)
         quantise_x2(4)
-        quantise_x(1)
         regroup_x2(5)
-        transposes(3)
-        interleave(3, 0, nc.scalar.copy)
-        interleave(3, 1, nc.scalar.copy)
+        quantise_x(1)
+        transposes(3, halves=(0,))
         stage1(4)
-        quantise_x(2)
+        transposes(3, halves=(1,))
+        interleave(3, 0, nc.scalar.copy)
         order3(4)
+        quantise_x(2)
         quantise_x2(5)
         regroup_x2(6)
 
         for i in range(1, B):
             stage2(i)
             finish(i)
+            interleave(i + 2, 1, nc.scalar.copy)
             quantise_x(i + 2)
             quantise_x2(i + 5)
             transposes(i + 3)
             interleave(i + 3, 0, nc.scalar.copy)
-            interleave(i + 3, 1, nc.scalar.copy)
             stage1(i + 4)
             order3(i + 4)
             regroup_x2(i + 6)

@@ -12,68 +12,64 @@ ALU = mybir.AluOpType
 
 P = 128
 B, N, D, O, M = 16, 512, 128, 512, 4
+PACK = 4
 T = N // P
-H = 2
-W2 = 2 * P
+HALF = N // 2
 FLOPS = 2 * B * N * N * D + 2 * B * N * (D * M) * O
 
-CHUNKS = [(0, 1), (1, 1), (2, 2), (4, 4), (8, 4), (12, 4)]
-SPLIT_FROM = 15
-GP1 = (0,)
-GP2 = (0, 2)
-TWO = ()
-V_REGROUPS = (0, 1, 2, 3)
-FILL = {(0, 0): 0, (0, 1): 0, (1, 0): 512, (1, 1): 512, (2, 0): 512, (2, 1): 0, (3, 0): 512, (3, 1): 0}
-FILL_LOOP = 128
-RING_FROM = 3
+CHUNKS = [(0, 1), (1, 1), (2, 2), (4, 2), (6, 2), (8, 4), (12, 4)]
+VECTOR_REGROUPS = 5
+SHARED_FROM = 4
+GPSIMD_TILE = 0
+BUSY_WIDE, BUSY_MIDDLE, BUSY_NARROW = 512, 256, 128
 
 
 def tile_dgcn_pb_t_kernel(tc, x0, x1, x2, support, weights, biases, out):
     nc = tc.nc
-    xs_dram = [x0, x1, x2]
+    x_dram = [x0, x1, x2]
     chunk_of = {}
-    for c, (b0, nb) in enumerate(CHUNKS):
-        for bi in range(nb):
-            chunk_of[b0 + bi] = (c, bi)
+    for c, (first, count) in enumerate(CHUNKS):
+        for at in range(count):
+            chunk_of[first + at] = (c, at)
 
     with ExitStack() as ctx:
         const = ctx.enter_context(tc.tile_pool(name="const", bufs=1))
         work = ctx.enter_context(tc.tile_pool(name="work", bufs=3))
-        outp = ctx.enter_context(tc.tile_pool(name="outp", bufs=5))
-        ps1 = ctx.enter_context(tc.psum_pool(name="ps1", bufs=1))
-        pst = ctx.enter_context(tc.psum_pool(name="pst", bufs=3))
-        ps2 = ctx.enter_context(tc.psum_pool(name="ps2", bufs=4))
+        results = ctx.enter_context(tc.tile_pool(name="results", bufs=5))
+        psum1 = ctx.enter_context(tc.psum_pool(name="psum1", bufs=1))
+        psum_x = ctx.enter_context(tc.psum_pool(name="psum_x", bufs=3))
+        psum2 = ctx.enter_context(tc.psum_pool(name="psum2", bufs=4))
         ctx.enter_context(tc.manual_schedule())
 
         x_sb = {}
 
         def load_x(m, c):
-            b0, nb = CHUNKS[c]
-            xt = const.tile([P, nb, T * D], BF16, name="x%d_c%d" % (m, c))
+            first, count = CHUNKS[c]
+            tile = const.tile([P, count, T * D], BF16, name="x%d_%d" % (m, c))
             nc.sync.dma_start(
-                out=xt[:], in_=xs_dram[m][b0 : b0 + nb].rearrange("b (p t) d -> p b (t d)", t=T)
+                out=tile[:], in_=x_dram[m][first : first + count].rearrange("b (p t) d -> p b (t d)", t=T)
             )
-            x_sb[(m, c)] = xt
+            x_sb[(m, c)] = tile
 
-        sup_sb = []
         bias_rows = const.tile([P, O], BF16)
-        ones_b = const.tile([P, P], BF16)
-        warm_rhs = const.tile([P, O], BF16)
-        nc.vector.memset(ones_b[:], 1.0)
-        nc.vector.memset(warm_rhs[:], 0.0)
+        ones = const.tile([P, P], BF16)
+        zeros = const.tile([P, O], BF16)
+        nc.vector.memset(ones[:], 1.0)
+        nc.vector.memset(zeros[:], 0.0)
         nc.vector.memset(bias_rows[:], 0.0)
 
-        def warm(n):
-            dum = ps2.tile([P, O], F32, name="dum", tag="acc2")
-            for k in range(n):
-                nc.tensor.matmul(dum[:], lhsT=ones_b[:], rhs=warm_rhs[:], start=True, stop=True)
+        def keep_busy(count):
+            dummy = psum2.tile([P, O], F32, name="dummy", tag="bank2")
+            for k in range(count):
+                nc.tensor.matmul(dummy[:], lhsT=ones[:], rhs=zeros[:], start=True, stop=True)
 
-        warm(4)
-        sup_view = support.rearrange("(p t) j -> p t j", t=T)
-        for h in range(H):
-            s_half = const.tile([P, 2, N], BF16, name="sup%d" % h)
-            nc.sync.dma_start(out=s_half[:], in_=sup_view[:, 2 * h : 2 * h + 2, :])
-            sup_sb.append(s_half)
+        keep_busy(4)
+        support_view = support.rearrange("(p t) j -> p t j", t=T)
+        support_sb = []
+        for h in range(2):
+            half = const.tile([P, 2, N], BF16, name="support%d" % h)
+            nc.sync.dma_start(out=half[:], in_=support_view[:, 2 * h : 2 * h + 2, :])
+            support_sb.append(half)
         load_x(2, 0)
         w_sb = const.tile([P, M * O], BF16)
         nc.sync.dma_start(out=bias_rows[0:1, :], in_=biases.rearrange("(a o) -> a o", a=1))
@@ -82,69 +78,71 @@ def tile_dgcn_pb_t_kernel(tc, x0, x1, x2, support, weights, biases, out):
         load_x(0, 0)
         load_x(2, 1)
         load_x(2, 2)
-        load_x(1, 1)
-        load_x(0, 1)
-        load_x(1, 2)
-        load_x(0, 2)
+        for c in (1, 2):
+            load_x(1, c)
+            load_x(0, c)
         for c in range(3, len(CHUNKS)):
             load_x(2, c)
             load_x(1, c)
             load_x(0, c)
 
-        ident_f = const.tile([P, P], F32)
-        make_identity(nc, ident_f[:])
-        ident_b = const.tile([P, P], BF16)
-        nc.vector.tensor_copy(out=ident_b[:], in_=ident_f[:])
+        ident_f32 = const.tile([P, P], F32)
+        make_identity(nc, ident_f32[:])
+        ident = const.tile([P, P], BF16)
+        nc.vector.tensor_copy(out=ident[:], in_=ident_f32[:])
 
-        x2g_t = {}
-        x2q_t = {}
+        x2_grouped = {}
+        x2_mx = {}
 
         def regroup_x2(b):
             if b >= B:
                 return
-            c, bi = chunk_of[b]
-            if b < RING_FROM:
-                x2g = const.tile([P, D, T], BF16, name="x2g_%d" % b, align_bytes=64)
+            c, at = chunk_of[b]
+            if b < SHARED_FROM:
+                grouped = const.tile([P, D, T], BF16, name="x2g_%d" % b, align_bytes=64)
             else:
-                x2g = const.tile([P, D, T], BF16, name="x2g_ring", tag="x2g_ring", align_bytes=64)
-            src = x_sb[(2, c)][:, bi, :].rearrange("p (t d) -> p d t", t=T)
-            if b in V_REGROUPS:
-                nc.vector.tensor_copy(out=x2g[:], in_=src)
+                grouped = const.tile([P, D, T], BF16, name="x2g_shared", tag="x2g_shared", align_bytes=64)
+            src = x_sb[(2, c)][:, at, :].rearrange("p (t d) -> p d t", t=T)
+            if b < VECTOR_REGROUPS:
+                nc.vector.tensor_copy(out=grouped[:], in_=src)
             else:
-                nc.gpsimd.tensor_scalar(out=x2g[:], in0=src, scalar1=1.0, scalar2=0.0, op0=ALU.mult, op1=ALU.add)
-            x2g_t[b] = x2g
+                nc.gpsimd.tensor_scalar(out=grouped[:], in0=src, scalar1=1.0, scalar2=0.0, op0=ALU.mult, op1=ALU.add)
+            x2_grouped[b] = grouped
 
         def quantise_x2(b):
             if b >= B:
                 return
             codes = const.tile([P, D], U32, name="x2c_%d" % b, align_bytes=64)
             scales = const.tile([P, D], U8, name="x2s_%d" % b, align_bytes=64)
-            nc.vector.quantize_mx(out=codes[:].bitcast(FP8X4), scales=scales[:], in_=x2g_t[b][:].rearrange("p d t -> p (d t)"))
-            x2q_t[b] = (codes, scales)
+            nc.vector.quantize_mx(
+                out=codes[:].bitcast(FP8X4), scales=scales[:], in_=x2_grouped[b][:].rearrange("p d t -> p (d t)")
+            )
+            x2_mx[b] = (codes, scales)
 
-        sg = const.tile([P, N * 4], BF16, align_bytes=64)
+        s_grouped = const.tile([P, N * PACK], BF16, align_bytes=64)
         s_codes = const.tile([P, N], U32, align_bytes=64)
         s_scales = const.tile([P, N], U8, align_bytes=64)
-        wg = const.tile([P, O * M], BF16, align_bytes=64)
+        w_grouped = const.tile([P, O * PACK], BF16, align_bytes=64)
         w_codes = const.tile([P, O], U32, align_bytes=64)
         w_scales = const.tile([P, O], U8, align_bytes=64)
         bias_sb = const.tile([P, O], F32)
-        x3_t = {}
-        acc1_t = {}
-        xg_t = {}
-        xq_t = {}
-        tp_t = {}
+        sums1 = {}
+        x3_sb = {}
+        xt_psum = {}
+        x_grouped = {}
+        x_mx = {}
+        sums2 = {}
 
-        def stage1(b, tiles=range(T)):
+        def diffuse(b, tiles=range(T)):
             if b >= B:
                 return
-            codes, scales = x2q_t[b]
-            if b not in acc1_t:
-                acc1 = ps1.tile([P, T * D], F32, name="acc1", tag="acc1")
-                acc1_t[b] = acc1
+            codes, scales = x2_mx[b]
+            if b not in sums1:
+                bank = psum1.tile([P, T * D], F32, name="bank1", tag="bank1")
+                sums1[b] = bank
             for t in tiles:
                 nc.tensor.matmul_mx(
-                    out=acc1_t[b][:, t * D : (t + 1) * D],
+                    out=sums1[b][:, t * D : (t + 1) * D],
                     lhsT=s_codes[:, t * P : (t + 1) * P].bitcast(FP8X4),
                     lhsT_scale=s_scales[:, t * P : (t + 1) * P],
                     rhs=codes[:].bitcast(FP8X4),
@@ -153,194 +151,199 @@ def tile_dgcn_pb_t_kernel(tc, x0, x1, x2, support, weights, biases, out):
                     stop=True,
                 )
 
-        def order3(b, lo=0, hi=T * D):
+        def make_x3(b, lo=0, hi=T * D):
             if b >= B:
                 return
-            c, bi = chunk_of[b]
-            if b not in x3_t:
+            c, at = chunk_of[b]
+            if b not in x3_sb:
                 x3 = work.tile([P, T * D], BF16, name="x3", tag="x3")
-                x3_t[b] = x3
+                x3_sb[b] = x3
             nc.vector.scalar_tensor_tensor(
-                out=x3_t[b][:, lo:hi], in0=acc1_t[b][:, lo:hi], scalar=2.0, in1=x_sb[(1, c)][:, bi, lo:hi],
-                op0=ALU.mult, op1=ALU.subtract,
+                out=x3_sb[b][:, lo:hi],
+                in0=sums1[b][:, lo:hi],
+                scalar=2.0,
+                in1=x_sb[(1, c)][:, at, lo:hi],
+                op0=ALU.mult,
+                op1=ALU.subtract,
             )
 
-        def transposes(b, orders=(0, 1, 2, 3), halves=(0, 1)):
+        def transpose_x(b, h, orders=range(M), busy=0):
             if b >= B:
                 return
-            c, bi = chunk_of[b]
-            for h in halves:
-                if (b, h) not in tp_t:
-                    tp = pst.tile([P, M, W2], BF16, name="tp", tag="tp")
-                    tp_t[(b, h)] = tp
-                fill = FILL.get((b, h), FILL_LOOP if h == 1 else 0)
-                if fill and 0 in orders:
-                    nc.tensor.matmul(
-                        tp_t[(b, h)][:].rearrange("p m c -> p (m c)")[:, :fill], lhsT=ones_b[:], rhs=warm_rhs[:, :fill], start=True, stop=True
-                    )
-                for m in orders:
-                    for tt in range(2):
-                        t = 2 * h + tt
-                        src = x_sb[(m, c)][:, bi, t * D : (t + 1) * D] if m < 3 else x3_t[b][:, t * D : (t + 1) * D]
-                        nc.tensor.transpose(tp_t[(b, h)][:, m, tt * P : (tt + 1) * P], src, ident_b[:])
+            c, at = chunk_of[b]
+            if (b, h) not in xt_psum:
+                bank = psum_x.tile([P, M, HALF], BF16, name="bank_x", tag="bank_x")
+                xt_psum[(b, h)] = bank
+            bank = xt_psum[(b, h)]
+            if busy:
+                nc.tensor.matmul(
+                    bank[:].rearrange("p m c -> p (m c)")[:, :busy],
+                    lhsT=ones[:],
+                    rhs=zeros[:, :busy],
+                    start=True,
+                    stop=True,
+                )
+            for m in orders:
+                for i in range(2):
+                    t = 2 * h + i
+                    src = x_sb[(m, c)][:, at, t * D : (t + 1) * D] if m < 3 else x3_sb[b][:, t * D : (t + 1) * D]
+                    nc.tensor.transpose(bank[:, m, i * P : (i + 1) * P], src, ident[:])
 
-        def interleave(b, h, copy, lo=0, hi=W2):
+        def interleave_x(b, h):
             if b >= B:
                 return
-            if b not in xg_t:
-                xg = work.tile([P, N, M], BF16, name="xg", tag="xg", align_bytes=64)
-                xg_t[b] = xg
-            copy(
-                out=xg_t[b][:, h * W2 + lo : h * W2 + hi, :],
-                in_=tp_t[(b, h)][:, :, lo:hi].rearrange("p m c -> p c m"),
+            if b not in x_grouped:
+                grouped = work.tile([P, N, M], BF16, name="xg", tag="xg", align_bytes=64)
+                x_grouped[b] = grouped
+            nc.scalar.copy(
+                out=x_grouped[b][:, h * HALF : (h + 1) * HALF, :], in_=xt_psum[(b, h)][:].rearrange("p m c -> p c m")
             )
 
         def quantise_x(b, lo=0, hi=N):
             if b >= B:
                 return
-            if b not in xq_t:
-                xc = work.tile([P, N], U32, name="xc", tag="xc", align_bytes=64)
-                xsc = work.tile([P, N], U8, name="xsc", tag="xsc", align_bytes=64)
-                xq_t[b] = (xc, xsc)
-            xc, xsc = xq_t[b]
+            if b not in x_mx:
+                codes = work.tile([P, N], U32, name="xc", tag="xc", align_bytes=64)
+                scales = work.tile([P, N], U8, name="xs", tag="xs", align_bytes=64)
+                x_mx[b] = (codes, scales)
+            codes, scales = x_mx[b]
             nc.vector.quantize_mx(
-                out=xc[:, lo:hi].bitcast(FP8X4), scales=xsc[:, lo:hi], in_=xg_t[b][:, lo:hi, :].rearrange("p c m -> p (c m)")
+                out=codes[:, lo:hi].bitcast(FP8X4),
+                scales=scales[:, lo:hi],
+                in_=x_grouped[b][:, lo:hi, :].rearrange("p c m -> p (c m)"),
             )
 
-        acc2_t = {}
-
-        def stage2(b, tiles=range(T)):
-            xc, xsc = xq_t[b]
-            for t in tiles:
-                acc2 = ps2.tile([P, O], F32, name="acc2", tag="acc2")
+        def project(b):
+            codes, scales = x_mx[b]
+            for t in range(T):
+                bank = psum2.tile([P, O], F32, name="bank2", tag="bank2")
                 nc.tensor.matmul_mx(
-                    out=acc2[:],
-                    lhsT=xc[:, t * P : (t + 1) * P].bitcast(FP8X4),
-                    lhsT_scale=xsc[:, t * P : (t + 1) * P],
+                    out=bank[:],
+                    lhsT=codes[:, t * P : (t + 1) * P].bitcast(FP8X4),
+                    lhsT_scale=scales[:, t * P : (t + 1) * P],
                     rhs=w_codes[:].bitcast(FP8X4),
                     rhs_scale=w_scales[:],
                     start=True,
                     stop=True,
                 )
-                acc2_t[(b, t)] = acc2
+                sums2[(b, t)] = bank
 
         def finish(b):
-            res = outp.tile([P, T, O], F32, name="res", tag="res")
-            out_b = out[b].rearrange("(p t) o -> p t o", t=T)
-            gp_banks = GP2 if b in TWO else GP1
-            for t in gp_banks:
-                tmp = work.tile([P, O], F32, name="tmp", tag="tmp")
-                nc.scalar.copy(out=tmp[:], in_=acc2_t[(b, t)][:])
-                nc.gpsimd.tensor_tensor(out=res[:, t, :], in0=tmp[:], in1=bias_sb[:], op=ALU.add)
+            result = results.tile([P, T, O], F32, name="result", tag="result")
+            copied = work.tile([P, O], F32, name="copied", tag="copied")
+            nc.scalar.copy(out=copied[:], in_=sums2[(b, GPSIMD_TILE)][:])
+            nc.gpsimd.tensor_tensor(out=result[:, GPSIMD_TILE, :], in0=copied[:], in1=bias_sb[:], op=ALU.add)
             for t in range(T):
-                if t not in gp_banks:
-                    nc.vector.tensor_tensor(out=res[:, t, :], in0=acc2_t[(b, t)][:], in1=bias_sb[:], op=ALU.add)
-                    if b >= SPLIT_FROM:
-                        nc.sync.dma_start(out=out_b[:, t, :], in_=res[:, t, :])
-            if b >= SPLIT_FROM:
-                for t in gp_banks:
-                    nc.sync.dma_start(out=out_b[:, t, :], in_=res[:, t, :])
-            else:
-                nc.sync.dma_start(out=out_b, in_=res[:])
+                if t != GPSIMD_TILE:
+                    nc.vector.tensor_tensor(out=result[:, t, :], in0=sums2[(b, t)][:], in1=bias_sb[:], op=ALU.add)
+            nc.sync.dma_start(out=out[b].rearrange("(p t) o -> p t o", t=T), in_=result[:])
 
-        sg_w = sg[:].bitcast(F32).rearrange("p (c u) -> p c u", u=2)
-        for h in range(H):
-            sup_w = sup_sb[h][:].rearrange("p t j -> p (t j)").bitcast(F32).rearrange("p (t i u) -> p t u i", t=2, u=2)
-            for tt in range(2):
-                sps = ps2.tile([P, 2, P], F32, name="sps", tag="acc2")
+        s_words = s_grouped[:].bitcast(F32).rearrange("p (c u) -> p c u", u=2)
+        for h in range(2):
+            words = support_sb[h][:].rearrange("p t j -> p (t j)").bitcast(F32).rearrange("p (t i u) -> p t u i", t=2, u=2)
+            for i in range(2):
+                t = 2 * h + i
+                pair = psum2.tile([P, 2, P], F32, name="pair", tag="bank2")
                 for u in range(2):
-                    nc.tensor.transpose(sps[:, u, :], sup_w[:, tt, u, :], ident_f[:])
-                src = sps[:].rearrange("p u c -> p c u")
-                t = 2 * h + tt
-                dst = sg_w[:, t * P : (t + 1) * P, :]
-                if tt == 0:
+                    nc.tensor.transpose(pair[:, u, :], words[:, i, u, :], ident_f32[:])
+                src = pair[:].rearrange("p u c -> p c u")
+                dst = s_words[:, t * P : (t + 1) * P, :]
+                if i == 0:
                     nc.vector.tensor_copy(out=dst, in_=src)
                     if h == 0:
                         regroup_x2(0)
                 else:
                     nc.scalar.copy(out=dst, in_=src)
-        w_view = w_sb[:].rearrange("p (j o) -> p o j", j=M)
-        wg_view = wg[:].rearrange("p (o j) -> p o j", j=M)
-        Q = O // 4
 
-        def regroup_w(k, engine):
-            g = slice(k * Q, (k + 1) * Q)
-            engine(out=wg_view[:, g, :], in_=w_view[:, g, :])
-
-        def quantise_s(h):
+        def quantise_support(h):
+            cols = slice(h * HALF, (h + 1) * HALF)
             nc.vector.quantize_mx(
-                out=s_codes[:, h * W2 : (h + 1) * W2].bitcast(FP8X4), scales=s_scales[:, h * W2 : (h + 1) * W2],
-                in_=sg[:, h * W2 * 4 : (h + 1) * W2 * 4],
+                out=s_codes[:, cols].bitcast(FP8X4),
+                scales=s_scales[:, cols],
+                in_=s_grouped[:, h * HALF * PACK : (h + 1) * HALF * PACK],
             )
 
-        warm(2)
-        bps = ps2.tile([P, O], F32, name="bps", tag="acc2")
-        nc.tensor.matmul(bps[:], lhsT=ones_b[:], rhs=bias_rows[:], start=True, stop=True)
+        w_from = w_sb[:].rearrange("p (j o) -> p o j", j=M)
+        w_to = w_grouped[:].rearrange("p (o j) -> p o j", j=M)
+
+        def regroup_w(quarter, copy):
+            cols = slice(quarter * P, (quarter + 1) * P)
+            copy(out=w_to[:, cols, :], in_=w_from[:, cols, :])
+
+        keep_busy(2)
+        bias_psum = psum2.tile([P, O], F32, name="bias_psum", tag="bank2")
+        nc.tensor.matmul(bias_psum[:], lhsT=ones[:], rhs=bias_rows[:], start=True, stop=True)
         regroup_w(0, nc.scalar.copy)
         regroup_w(1, nc.scalar.copy)
-        nc.scalar.copy(out=bias_sb[:], in_=bps[:])
+        nc.scalar.copy(out=bias_sb[:], in_=bias_psum[:])
+
         quantise_x2(0)
-        quantise_s(0)
-        stage1(0, (0, 1))
-        warm(2)
+        quantise_support(0)
+        diffuse(0, (0, 1))
+        keep_busy(2)
         regroup_w(2, nc.vector.tensor_copy)
-        quantise_s(1)
-        order3(0, 0, W2)
+        quantise_support(1)
+        make_x3(0, 0, HALF)
         regroup_w(3, nc.vector.tensor_copy)
-        transposes(0, (0, 1, 2), (0, 1))
-        transposes(0, (3,), (0,))
-        interleave(0, 0, nc.scalar.copy)
-        stage1(0, (2, 3))
-        warm(2)
+        transpose_x(0, 0, (0, 1, 2))
+        transpose_x(0, 1, (0, 1, 2))
+        transpose_x(0, 0, (3,))
+        interleave_x(0, 0)
+        diffuse(0, (2, 3))
+        keep_busy(2)
         regroup_x2(1)
         quantise_x2(1)
-        order3(0, W2, 2 * W2)
-        nc.vector.quantize_mx(out=w_codes[:].bitcast(FP8X4), scales=w_scales[:], in_=wg[:])
-        transposes(0, (3,), (1,))
-        interleave(0, 1, nc.scalar.copy)
-        stage1(1)
-        warm(1)
-        quantise_x(0, 0, W2)
-        order3(1)
-        for b in range(2, 4):
-            regroup_x2(b)
-        transposes(1)
-        interleave(1, 0, nc.scalar.copy)
-        interleave(1, 1, nc.scalar.copy)
+        make_x3(0, HALF, 2 * HALF)
+        nc.vector.quantize_mx(out=w_codes[:].bitcast(FP8X4), scales=w_scales[:], in_=w_grouped[:])
+        transpose_x(0, 1, (3,))
+        interleave_x(0, 1)
+        diffuse(1)
+        keep_busy(1)
+        quantise_x(0, 0, HALF)
+        make_x3(1)
+        regroup_x2(2)
+        regroup_x2(3)
+        transpose_x(1, 0, busy=BUSY_WIDE)
+        transpose_x(1, 1)
+        interleave_x(1, 0)
+        interleave_x(1, 1)
         quantise_x2(2)
-        stage1(2)
-        quantise_x(0, W2, N)
-        order3(2)
-        stage2(0)
-        quantise_x2(3)
+        diffuse(2)
+        quantise_x(0, HALF, N)
         regroup_x2(4)
-        transposes(2, halves=(0,))
-        stage1(3)
-        transposes(2, halves=(1,))
-        finish(0)
-        interleave(2, 0, nc.scalar.copy)
-        interleave(2, 1, nc.scalar.copy)
-        order3(3)
+        make_x3(2)
+        project(0)
+        quantise_x2(3)
         quantise_x2(4)
         regroup_x2(5)
-        quantise_x(1)
-        transposes(3, halves=(0,))
-        stage1(4)
-        transposes(3, halves=(1,))
-        interleave(3, 0, nc.scalar.copy)
-        order3(4)
-        quantise_x(2)
+        transpose_x(2, 0, busy=BUSY_MIDDLE)
+        diffuse(3)
+        transpose_x(2, 1)
+        finish(0)
+        interleave_x(2, 0)
+        interleave_x(2, 1)
+        make_x3(3)
         quantise_x2(5)
         regroup_x2(6)
+        quantise_x(1)
+        transpose_x(3, 0, busy=BUSY_WIDE)
+        diffuse(4)
+        transpose_x(3, 1)
+        interleave_x(3, 0)
+        make_x3(4)
+        quantise_x(2)
+        quantise_x2(6)
+        regroup_x2(7)
 
         for i in range(1, B):
-            stage2(i)
+            project(i)
             finish(i)
-            interleave(i + 2, 1, nc.scalar.copy)
+            interleave_x(i + 2, 1)
             quantise_x(i + 2)
-            quantise_x2(i + 5)
-            transposes(i + 3)
-            interleave(i + 3, 0, nc.scalar.copy)
-            stage1(i + 4)
-            order3(i + 4)
-            regroup_x2(i + 6)
+            quantise_x2(i + 6)
+            transpose_x(i + 3, 0)
+            transpose_x(i + 3, 1, busy=BUSY_NARROW)
+            interleave_x(i + 3, 0)
+            diffuse(i + 4)
+            make_x3(i + 4)
+            regroup_x2(i + 7)

from contextlib import ExitStack

import concourse.mybir as mybir
from concourse.masks import make_identity

F32 = mybir.dt.float32
BF16 = mybir.dt.bfloat16
U32 = mybir.dt.uint32
U8 = mybir.dt.uint8
FP8X4 = mybir.dt.float8_e4m3fn_x4
ALU = mybir.AluOpType

P = 128
B, N, D, O, M = 16, 512, 128, 512, 4
PACK = 4
T = N // P
HALF = N // 2
FLOPS = 2 * B * N * N * D + 2 * B * N * (D * M) * O

CHUNKS = [(0, 1), (1, 1), (2, 2), (4, 2), (6, 2), (8, 4), (12, 4)]
VECTOR_REGROUPS = 5
SHARED_FROM = 4
GPSIMD_TILE = 0
BUSY_WIDE, BUSY_MIDDLE, BUSY_NARROW = 512, 256, 128


def tile_dgcn_pb_t_kernel(tc, x0, x1, x2, support, weights, biases, out):
    nc = tc.nc
    x_dram = [x0, x1, x2]
    chunk_of = {}
    for c, (first, count) in enumerate(CHUNKS):
        for at in range(count):
            chunk_of[first + at] = (c, at)

    with ExitStack() as ctx:
        const = ctx.enter_context(tc.tile_pool(name="const", bufs=1))
        work = ctx.enter_context(tc.tile_pool(name="work", bufs=3))
        results = ctx.enter_context(tc.tile_pool(name="results", bufs=5))
        psum1 = ctx.enter_context(tc.psum_pool(name="psum1", bufs=1))
        psum_x = ctx.enter_context(tc.psum_pool(name="psum_x", bufs=3))
        psum2 = ctx.enter_context(tc.psum_pool(name="psum2", bufs=4))
        ctx.enter_context(tc.manual_schedule())

        x_sb = {}

        def load_x(m, c):
            first, count = CHUNKS[c]
            tile = const.tile([P, count, T * D], BF16, name="x%d_%d" % (m, c))
            nc.sync.dma_start(
                out=tile[:], in_=x_dram[m][first : first + count].rearrange("b (p t) d -> p b (t d)", t=T)
            )
            x_sb[(m, c)] = tile

        bias_rows = const.tile([P, O], BF16)
        ones = const.tile([P, P], BF16)
        zeros = const.tile([P, O], BF16)
        nc.vector.memset(ones[:], 1.0)
        nc.vector.memset(zeros[:], 0.0)
        nc.vector.memset(bias_rows[:], 0.0)

        def keep_busy(count):
            dummy = psum2.tile([P, O], F32, name="dummy", tag="bank2")
            for k in range(count):
                nc.tensor.matmul(dummy[:], lhsT=ones[:], rhs=zeros[:], start=True, stop=True)

        keep_busy(4)
        support_view = support.rearrange("(p t) j -> p t j", t=T)
        support_sb = []
        for h in range(2):
            half = const.tile([P, 2, N], BF16, name="support%d" % h)
            nc.sync.dma_start(out=half[:], in_=support_view[:, 2 * h : 2 * h + 2, :])
            support_sb.append(half)
        load_x(2, 0)
        w_sb = const.tile([P, M * O], BF16)
        nc.sync.dma_start(out=bias_rows[0:1, :], in_=biases.rearrange("(a o) -> a o", a=1))
        nc.sync.dma_start(out=w_sb[:], in_=weights.rearrange("(p j) o -> p (j o)", j=M))
        load_x(1, 0)
        load_x(0, 0)
        load_x(2, 1)
        load_x(2, 2)
        for c in (1, 2):
            load_x(1, c)
            load_x(0, c)
        for c in range(3, len(CHUNKS)):
            load_x(2, c)
            load_x(1, c)
            load_x(0, c)

        ident_f32 = const.tile([P, P], F32)
        make_identity(nc, ident_f32[:])
        ident = const.tile([P, P], BF16)
        nc.vector.tensor_copy(out=ident[:], in_=ident_f32[:])

        x2_grouped = {}
        x2_mx = {}

        def regroup_x2(b):
            if b >= B:
                return
            c, at = chunk_of[b]
            if b < SHARED_FROM:
                grouped = const.tile([P, D, T], BF16, name="x2g_%d" % b, align_bytes=64)
            else:
                grouped = const.tile([P, D, T], BF16, name="x2g_shared", tag="x2g_shared", align_bytes=64)
            src = x_sb[(2, c)][:, at, :].rearrange("p (t d) -> p d t", t=T)
            if b < VECTOR_REGROUPS:
                nc.vector.tensor_copy(out=grouped[:], in_=src)
            else:
                nc.gpsimd.tensor_scalar(out=grouped[:], in0=src, scalar1=1.0, scalar2=0.0, op0=ALU.mult, op1=ALU.add)
            x2_grouped[b] = grouped

        def quantise_x2(b):
            if b >= B:
                return
            codes = const.tile([P, D], U32, name="x2c_%d" % b, align_bytes=64)
            scales = const.tile([P, D], U8, name="x2s_%d" % b, align_bytes=64)
            nc.vector.quantize_mx(
                out=codes[:].bitcast(FP8X4), scales=scales[:], in_=x2_grouped[b][:].rearrange("p d t -> p (d t)")
            )
            x2_mx[b] = (codes, scales)

        s_grouped = const.tile([P, N * PACK], BF16, align_bytes=64)
        s_codes = const.tile([P, N], U32, align_bytes=64)
        s_scales = const.tile([P, N], U8, align_bytes=64)
        w_grouped = const.tile([P, O * PACK], BF16, align_bytes=64)
        w_codes = const.tile([P, O], U32, align_bytes=64)
        w_scales = const.tile([P, O], U8, align_bytes=64)
        bias_sb = const.tile([P, O], F32)
        sums1 = {}
        x3_sb = {}
        xt_psum = {}
        x_grouped = {}
        x_mx = {}
        sums2 = {}

        def diffuse(b, tiles=range(T)):
            if b >= B:
                return
            codes, scales = x2_mx[b]
            if b not in sums1:
                bank = psum1.tile([P, T * D], F32, name="bank1", tag="bank1")
                sums1[b] = bank
            for t in tiles:
                nc.tensor.matmul_mx(
                    out=sums1[b][:, t * D : (t + 1) * D],
                    lhsT=s_codes[:, t * P : (t + 1) * P].bitcast(FP8X4),
                    lhsT_scale=s_scales[:, t * P : (t + 1) * P],
                    rhs=codes[:].bitcast(FP8X4),
                    rhs_scale=scales[:],
                    start=True,
                    stop=True,
                )

        def make_x3(b, lo=0, hi=T * D):
            if b >= B:
                return
            c, at = chunk_of[b]
            if b not in x3_sb:
                x3 = work.tile([P, T * D], BF16, name="x3", tag="x3")
                x3_sb[b] = x3
            nc.vector.scalar_tensor_tensor(
                out=x3_sb[b][:, lo:hi],
                in0=sums1[b][:, lo:hi],
                scalar=2.0,
                in1=x_sb[(1, c)][:, at, lo:hi],
                op0=ALU.mult,
                op1=ALU.subtract,
            )

        def transpose_x(b, h, orders=range(M), busy=0):
            if b >= B:
                return
            c, at = chunk_of[b]
            if (b, h) not in xt_psum:
                bank = psum_x.tile([P, M, HALF], BF16, name="bank_x", tag="bank_x")
                xt_psum[(b, h)] = bank
            bank = xt_psum[(b, h)]
            if busy:
                nc.tensor.matmul(
                    bank[:].rearrange("p m c -> p (m c)")[:, :busy],
                    lhsT=ones[:],
                    rhs=zeros[:, :busy],
                    start=True,
                    stop=True,
                )
            for m in orders:
                for i in range(2):
                    t = 2 * h + i
                    src = x_sb[(m, c)][:, at, t * D : (t + 1) * D] if m < 3 else x3_sb[b][:, t * D : (t + 1) * D]
                    nc.tensor.transpose(bank[:, m, i * P : (i + 1) * P], src, ident[:])

        def interleave_x(b, h):
            if b >= B:
                return
            if b not in x_grouped:
                grouped = work.tile([P, N, M], BF16, name="xg", tag="xg", align_bytes=64)
                x_grouped[b] = grouped
            nc.scalar.copy(
                out=x_grouped[b][:, h * HALF : (h + 1) * HALF, :], in_=xt_psum[(b, h)][:].rearrange("p m c -> p c m")
            )

        def quantise_x(b, lo=0, hi=N):
            if b >= B:
                return
            if b not in x_mx:
                codes = work.tile([P, N], U32, name="xc", tag="xc", align_bytes=64)
                scales = work.tile([P, N], U8, name="xs", tag="xs", align_bytes=64)
                x_mx[b] = (codes, scales)
            codes, scales = x_mx[b]
            nc.vector.quantize_mx(
                out=codes[:, lo:hi].bitcast(FP8X4),
                scales=scales[:, lo:hi],
                in_=x_grouped[b][:, lo:hi, :].rearrange("p c m -> p (c m)"),
            )

        def project(b):
            codes, scales = x_mx[b]
            for t in range(T):
                bank = psum2.tile([P, O], F32, name="bank2", tag="bank2")
                nc.tensor.matmul_mx(
                    out=bank[:],
                    lhsT=codes[:, t * P : (t + 1) * P].bitcast(FP8X4),
                    lhsT_scale=scales[:, t * P : (t + 1) * P],
                    rhs=w_codes[:].bitcast(FP8X4),
                    rhs_scale=w_scales[:],
                    start=True,
                    stop=True,
                )
                sums2[(b, t)] = bank

        def finish(b):
            result = results.tile([P, T, O], F32, name="result", tag="result")
            copied = work.tile([P, O], F32, name="copied", tag="copied")
            nc.scalar.copy(out=copied[:], in_=sums2[(b, GPSIMD_TILE)][:])
            nc.gpsimd.tensor_tensor(out=result[:, GPSIMD_TILE, :], in0=copied[:], in1=bias_sb[:], op=ALU.add)
            for t in range(T):
                if t != GPSIMD_TILE:
                    nc.vector.tensor_tensor(out=result[:, t, :], in0=sums2[(b, t)][:], in1=bias_sb[:], op=ALU.add)
            nc.sync.dma_start(out=out[b].rearrange("(p t) o -> p t o", t=T), in_=result[:])

        s_words = s_grouped[:].bitcast(F32).rearrange("p (c u) -> p c u", u=2)
        for h in range(2):
            words = support_sb[h][:].rearrange("p t j -> p (t j)").bitcast(F32).rearrange("p (t i u) -> p t u i", t=2, u=2)
            for i in range(2):
                t = 2 * h + i
                pair = psum2.tile([P, 2, P], F32, name="pair", tag="bank2")
                for u in range(2):
                    nc.tensor.transpose(pair[:, u, :], words[:, i, u, :], ident_f32[:])
                src = pair[:].rearrange("p u c -> p c u")
                dst = s_words[:, t * P : (t + 1) * P, :]
                if i == 0:
                    nc.vector.tensor_copy(out=dst, in_=src)
                    if h == 0:
                        regroup_x2(0)
                else:
                    nc.scalar.copy(out=dst, in_=src)

        def quantise_support(h):
            cols = slice(h * HALF, (h + 1) * HALF)
            nc.vector.quantize_mx(
                out=s_codes[:, cols].bitcast(FP8X4),
                scales=s_scales[:, cols],
                in_=s_grouped[:, h * HALF * PACK : (h + 1) * HALF * PACK],
            )

        w_from = w_sb[:].rearrange("p (j o) -> p o j", j=M)
        w_to = w_grouped[:].rearrange("p (o j) -> p o j", j=M)

        def regroup_w(quarter, copy):
            cols = slice(quarter * P, (quarter + 1) * P)
            copy(out=w_to[:, cols, :], in_=w_from[:, cols, :])

        keep_busy(2)
        bias_psum = psum2.tile([P, O], F32, name="bias_psum", tag="bank2")
        nc.tensor.matmul(bias_psum[:], lhsT=ones[:], rhs=bias_rows[:], start=True, stop=True)
        regroup_w(0, nc.scalar.copy)
        regroup_w(1, nc.scalar.copy)
        nc.scalar.copy(out=bias_sb[:], in_=bias_psum[:])

        quantise_x2(0)
        quantise_support(0)
        diffuse(0, (0, 1))
        keep_busy(2)
        regroup_w(2, nc.vector.tensor_copy)
        quantise_support(1)
        make_x3(0, 0, HALF)
        regroup_w(3, nc.vector.tensor_copy)
        transpose_x(0, 0, (0, 1, 2))
        transpose_x(0, 1, (0, 1, 2))
        transpose_x(0, 0, (3,))
        interleave_x(0, 0)
        diffuse(0, (2, 3))
        keep_busy(2)
        regroup_x2(1)
        quantise_x2(1)
        make_x3(0, HALF, 2 * HALF)
        nc.vector.quantize_mx(out=w_codes[:].bitcast(FP8X4), scales=w_scales[:], in_=w_grouped[:])
        transpose_x(0, 1, (3,))
        interleave_x(0, 1)
        diffuse(1)
        keep_busy(1)
        quantise_x(0, 0, HALF)
        make_x3(1)
        regroup_x2(2)
        regroup_x2(3)
        transpose_x(1, 0, busy=BUSY_WIDE)
        transpose_x(1, 1)
        interleave_x(1, 0)
        interleave_x(1, 1)
        quantise_x2(2)
        diffuse(2)
        quantise_x(0, HALF, N)
        regroup_x2(4)
        make_x3(2)
        project(0)
        quantise_x2(3)
        quantise_x2(4)
        regroup_x2(5)
        transpose_x(2, 0, busy=BUSY_MIDDLE)
        diffuse(3)
        transpose_x(2, 1)
        finish(0)
        interleave_x(2, 0)
        interleave_x(2, 1)
        make_x3(3)
        quantise_x2(5)
        regroup_x2(6)
        quantise_x(1)
        transpose_x(3, 0, busy=BUSY_WIDE)
        diffuse(4)
        transpose_x(3, 1)
        interleave_x(3, 0)
        make_x3(4)
        quantise_x(2)
        quantise_x2(6)
        regroup_x2(7)

        for i in range(1, B):
            project(i)
            finish(i)
            interleave_x(i + 2, 1)
            quantise_x(i + 2)
            quantise_x2(i + 6)
            transpose_x(i + 3, 0)
            transpose_x(i + 3, 1, busy=BUSY_NARROW)
            interleave_x(i + 3, 0)
            diffuse(i + 4)
            make_x3(i + 4)
            regroup_x2(i + 7)
